import numpy as np
import ml_dtypes


def mxq(x, axis, fmt="e4m3"):
    dtype, down = {"e4m3": (ml_dtypes.float8_e4m3fn, 7), "e5m2": (ml_dtypes.float8_e5m2, 14)}[fmt]
    v = np.moveaxis(np.asarray(x, np.float32).astype(ml_dtypes.bfloat16).astype(np.float64), axis, -1)
    blocks = v.reshape(v.shape[:-1] + (-1, 32))
    amax = np.abs(blocks).max(-1, keepdims=True)
    byte = np.maximum(np.where(amax > 0, np.frexp(amax)[1] - 1 + 127, 0) - down, 1)
    scale = np.exp2(byte - 127.0)
    codes = (blocks / scale).astype(np.float32).astype(dtype).astype(np.float64)
    return np.moveaxis((codes * scale).reshape(v.shape), -1, axis)


WIDE = False


def mx_kscale(k):
    if not WIDE:
        return np.ones(k)
    levels = np.array([10, -10, 5, -5, 0])
    if k % 512:
        return np.exp2(np.random.permutation(np.resize(levels, k // 32))).repeat(32)
    a = np.empty((k // 512, 16))
    for p in range(k // 512):
        a[p, :8] = np.random.permutation(np.resize(levels, 8))
        for g in range(8):
            far = levels[np.abs(levels - a[p, g]) >= 10]
            a[p, g + 8] = far[np.random.randint(len(far))]
    return np.exp2(a.ravel()).repeat(32)


BF16 = ml_dtypes.bfloat16


def bf(x):
    return np.asarray(x, np.float32).astype(BF16)


def f64(x):
    return np.asarray(x).astype(np.float64)


B, T, FS, H, HD = 1, 1024, 512, 12, 128
D = H * HD
EPS = 1e-6
ROPE_BASE = 10000.0


def rmsnorm(u, g):
    var = np.mean(u * u, axis=-1, keepdims=True)
    return u * (1.0 / np.sqrt(var + EPS)) * g


def rope(u, cos, sin):
    ur = u.reshape(B, T, H, HD // 2, 2)
    a, b = ur[..., 0], ur[..., 1]
    c = cos[None, :, None, :]
    s = sin[None, :, None, :]
    return np.stack([a * c - b * s, a * s + b * c], axis=-1).reshape(B, T, H, HD)


def draw0():
    s = mx_kscale(D)
    inv = ROPE_BASE ** (-np.arange(HD // 2) / (HD // 2))
    ang = np.arange(T)[:, None] * inv[None, :]
    return {"x": bf(np.random.standard_normal((B, T, D)) * s),
            "w": bf(np.random.standard_normal((D, D)) / np.sqrt(D) / s[:, None]),
            "b": bf(np.random.standard_normal(D) * 0.1),
            "g": bf(1.0 + 0.1 * np.random.standard_normal(D)),
            "freqs_cos": bf(np.cos(ang)),
            "freqs_sin": bf(np.sin(ang))}


def core(x, w, b, g, freqs_cos, freqs_sin):
    u = (mxq(f64(x), 2, "e4m3") @ mxq(f64(w), 0, "e4m3")) + f64(b)
    return rope(rmsnorm(u, f64(g)).reshape(B, T, H, HD), f64(freqs_cos), f64(freqs_sin))


def e4m3fn_bytes(y):
    return np.clip(np.asarray(y, np.float64), -448.0, 448.0).astype(np.float32).astype(ml_dtypes.float8_e4m3fn).view(np.uint8)


def e4m3fn_values(b):
    return np.asarray(b, np.uint8).view(ml_dtypes.float8_e4m3fn).astype(np.float64)


def setup_inputs():
    d = draw0()
    x0 = np.asarray(d['w']).astype(np.float64)
    s = (np.max(np.abs(x0), axis=(1,), keepdims=True) / 448.0).astype(np.float32)
    out = {}
    for k, v in d.items():
        if k == 'w':
            out['w_bytes'] = e4m3fn_bytes(x0 / s.astype(np.float64))
            out['w_scale'] = s
        else:
            out[k] = v
    return out


def reference(x, w_bytes, w_scale, b, g, freqs_cos, freqs_sin):
    return core(x, e4m3fn_values(w_bytes) * w_scale.astype(np.float64), b, g, freqs_cos, freqs_sin)

@@ -1,0 +1,258 @@
+from contextlib import ExitStack
+
+import concourse.mybir as mybir
+from concourse.masks import make_identity
+
+F32 = mybir.dt.float32
+BF16 = mybir.dt.bfloat16
+U32 = mybir.dt.uint32
+U8 = mybir.dt.uint8
+FP8 = mybir.dt.float8_e4m3fn
+FP8X4 = mybir.dt.float8_e4m3fn_x4
+ALU = mybir.AluOpType
+ACT = mybir.ActivationFunctionType
+AX = mybir.AxisListType
+
+T = 1024
+D = 1536
+H = 12
+J = 64
+P = 128
+PACK = 4
+K_PASS = P * PACK
+G = D // K_PASS
+NCH = 512
+TT = T // P
+XU = 256
+EPS = 1e-6
+FLOPS = 2 * T * D * D
+CHUNKS = ((0, 1), (1, 2), (3, 2), (5, 2), (7, 1))
+W_BLOCKS = ((0, 4), (4, 4), (8, 2), (10, 2))
+
+
+def tile_causalwanmodel_pa_kernel(tc, x, w_bytes, w_scale, b, g, freqs_cos, freqs_sin, out):
+    nc = tc.nc
+    x_rows = x.rearrange("o t k -> (o t) k")
+    out_rows = out.rearrange("o t h d -> (o t) (h d)")
+    w_view = w_bytes.rearrange("(g p t) n -> g p t n", p=P, t=PACK)
+
+    with ExitStack() as ctx:
+        keep = ctx.enter_context(tc.tile_pool(name="keep", bufs=1))
+        stage = ctx.enter_context(tc.tile_pool(name="stage", bufs=3))
+        vpool = ctx.enter_context(tc.tile_pool(name="vpool", bufs=3))
+        sqp = ctx.enter_context(tc.tile_pool(name="sqp", bufs=2))
+        epi = ctx.enter_context(tc.tile_pool(name="epi", bufs=3))
+        ps_t = ctx.enter_context(tc.psum_pool(name="ps_t", bufs=4))
+        ps_a = ctx.enter_context(tc.psum_pool(name="ps_a", bufs=3))
+        ps_s = ctx.enter_context(tc.psum_pool(name="ps_s", bufs=1))
+
+        cos_sb = keep.tile([P, TT, J], BF16, name="cos_sb")
+        sin_sb = keep.tile([P, TT, J], BF16, name="sin_sb")
+        nc.scalar.dma_start(out=cos_sb[:], in_=freqs_cos.rearrange("(i p) j -> p i j", p=P))
+        nc.scalar.dma_start(out=sin_sb[:], in_=freqs_sin.rearrange("(i p) j -> p i j", p=P))
+        bg_rows = keep.tile([P, P], BF16, name="bg_rows")
+        nc.vector.memset(bg_rows[:], 0.0)
+        nc.scalar.dma_start(out=bg_rows[0:H, :], in_=b.rearrange("(h p) -> h p", p=P))
+        nc.scalar.dma_start(out=bg_rows[32:32 + H, :], in_=g.rearrange("(h p) -> h p", p=P))
+
+        wsc = keep.tile([P, G, PACK], F32, name="wsc")
+        nc.sync.dma_start(out=wsc[:], in_=w_scale.rearrange("(g p t) o -> p g (t o)", p=P, t=PACK))
+        wb = keep.tile([P, G, PACK, D], U8, name="w_bytes_sb")
+        x_sb = keep.tile([P, TT, D], BF16, name="x_sb")
+
+        def load_w(c):
+            for gg in range(G):
+                nc.sync.dma_start(out=wb[:, gg, :, c * NCH:(c + 1) * NCH], in_=w_view[gg][:, :, c * NCH:(c + 1) * NCH])
+
+        def load_x(i):
+            nc.sync.dma_start(out=x_sb[:, i, :], in_=x_rows[i * P:(i + 1) * P, :])
+
+        load_w(0)
+        load_x(0)
+        load_x(1)
+        load_w(1)
+        load_w(2)
+        for i in range(2, TT):
+            load_x(i)
+
+        sgn = keep.tile([P, 2], F32, name="sgn")
+        nc.vector.memset(sgn[:, 0:1], -1.0)
+        nc.vector.memset(sgn[:, 1:2], 1.0)
+        eps_t = keep.tile([P, 1], F32, name="eps_t")
+        nc.vector.memset(eps_t[:], EPS)
+        warm = keep.tile([P, 1], F32, name="warm")
+        nc.scalar.activation(out=warm[:], in_=sgn[:, 1:2], func=ACT.Sqrt)
+        ident = keep.tile([P, P], F32, name="ident")
+        make_identity(nc, ident[:])
+
+        cdup = keep.tile([P, TT * J, 2], F32, name="cdup")
+        s3 = keep.tile([P, TT * J, 2], F32, name="s3")
+        nc.vector.tensor_copy(out=cdup[:], in_=cos_sb[:].rearrange("p i j -> p (i j)").unsqueeze(2).to_broadcast([P, TT * J, 2]))
+        nc.vector.tensor_tensor(
+            out=s3[:], in0=sin_sb[:].rearrange("p i j -> p (i j)").unsqueeze(2).to_broadcast([P, TT * J, 2]),
+            in1=sgn[:].unsqueeze(1).to_broadcast([P, TT * J, 2]), op=ALU.mult,
+        )
+
+        bg_f = keep.tile([P, P], F32, name="bg_f")
+        nc.vector.tensor_copy(out=bg_f[:], in_=bg_rows[:])
+        bg_ps = ps_t.tile([P, P], F32, name="bg_ps", tag="tp")
+        nc.tensor.transpose(bg_ps[:], bg_f[:], ident[:])
+        bgc = keep.tile([P, P], F32, name="bgc")
+        nc.vector.tensor_copy(out=bgc[:], in_=bg_ps[:])
+        gb = keep.tile([P, H], F32, name="gb")
+        nc.vector.tensor_tensor(out=gb[:], in0=bgc[:, 0:H], in1=bgc[:, 32:32 + H], op=ALU.mult)
+
+        w_codes = keep.tile([P, G, D], U32, name="w_codes", align_bytes=64)
+        w_scl = keep.tile([P, G, D], U8, name="w_scl", align_bytes=64)
+        x_codes = keep.tile([P, G, T], U32, name="x_codes", align_bytes=64)
+        x_scl = keep.tile([P, G, T], U8, name="x_scl", align_bytes=64)
+
+        def x_front(xu):
+            xs = slice(xu * XU, (xu + 1) * XU)
+            for gg in range(G):
+                xt = ps_t.tile([P, 2, XU], F32, name="xt", tag="tp")
+                for r in range(2):
+                    words = x_sb[:, 2 * xu + r, :].bitcast(F32)
+                    for u in range(2):
+                        nc.tensor.transpose(xt[:, u, r * P:(r + 1) * P], words[:, 256 * gg + u:256 * (gg + 1):2], ident[:])
+                xg = stage.tile([P, XU * PACK], BF16, name="xg", align_bytes=64)
+                nc.scalar.copy(out=xg[:].bitcast(F32).rearrange("p (r u) -> p r u", u=2), in_=xt[:].rearrange("p u r -> p r u"))
+                nc.vector.quantize_mx(out=x_codes[:, gg, xs].bitcast(FP8X4), scales=x_scl[:, gg, xs], in_=xg[:])
+
+        def w_copy(h0, nh, gg):
+            cs = slice(h0 * P, (h0 + nh) * P)
+            wide = stage.tile([P, PACK, nh * P], BF16, name="wide")
+            for t in range(PACK):
+                src = wb[:, gg, t, cs].bitcast(FP8)
+                if t == 3:
+                    nc.vector.tensor_scalar(out=wide[:, t, :], in0=src, scalar1=wsc[:, gg, t:t + 1], scalar2=None, op0=ALU.mult)
+                else:
+                    nc.scalar.activation(out=wide[:, t, :], in_=src, func=ACT.Copy, scale=wsc[:, gg, t:t + 1])
+            wg = stage.tile([P, nh * P, PACK], BF16, name="wg", align_bytes=64)
+            nc.vector.tensor_copy(out=wg[:].rearrange("p (c i) t -> p c t i", i=4), in_=wide[:].rearrange("p t (c i) -> p c t i", i=4))
+            return wg
+
+        def w_quant(h0, nh, gg, wg):
+            cs = slice(h0 * P, (h0 + nh) * P)
+            nc.vector.quantize_mx(out=w_codes[:, gg, cs].bitcast(FP8X4), scales=w_scl[:, gg, cs], in_=wg[:].rearrange("p n t -> p (n t)"))
+
+        ss_ps = ps_s.tile([P, 4, P], F32, name="ss_ps")
+        ms = keep.tile([P, TT], F32, name="ms")
+        rstd = keep.tile([P, TT], F32, name="rstd")
+
+        def mx(t0, nt, hp):
+            acc = ps_a.tile([P, 2, nt * P], F32, name="acc")
+            ts = slice(t0 * P, (t0 + nt) * P)
+            for a in range(2):
+                hs = slice((2 * hp + a) * P, (2 * hp + a + 1) * P)
+                for gg in range(G):
+                    nc.tensor.matmul_mx(
+                        out=acc[:, a, :],
+                        lhsT=w_codes[:, gg, hs].bitcast(FP8X4), lhsT_scale=w_scl[:, gg, hs],
+                        rhs=x_codes[:, gg, ts].bitcast(FP8X4), rhs_scale=x_scl[:, gg, ts],
+                        start=(gg == 0), stop=(gg == G - 1),
+                    )
+            return acc
+
+        def ev(hp, acc, v_k, sq_k, v_on_vector):
+            for a in range(2):
+                h = 2 * hp + a
+                nc.scalar.activation(out=sq_k[:, h, :], in_=acc[:, a, :], func=ACT.Square, bias=bgc[:, h:h + 1])
+                if v_on_vector and h % 3 == 0:
+                    nc.vector.tensor_scalar(out=v_k[:, h, :], in0=acc[:, a, :], scalar1=bgc[:, 32 + h:33 + h], scalar2=gb[:, h:h + 1], op0=ALU.mult, op1=ALU.add)
+                else:
+                    nc.scalar.activation(out=v_k[:, h, :], in_=acc[:, a, :], func=ACT.Identity, scale=bgc[:, 32 + h:33 + h], bias=gb[:, h:h + 1])
+
+        def ssq(nt, sq_k, heads, base):
+            for r in range(nt):
+                for h in heads:
+                    nc.tensor.matmul(out=ss_ps[:, base + r, :], lhsT=sq_k[:, h, r * P:(r + 1) * P], rhs=ident[:], is_transpose=True, start=(h == 0), stop=(h == H - 1))
+
+        def rsqrt(isl):
+            nc.scalar.activation(out=ms[:, isl], in_=ms[:, isl], func=ACT.Sqrt, scale=1.0 / D, bias=eps_t[:])
+            nc.vector.reciprocal(out=rstd[:, isl], in_=ms[:, isl])
+
+        def norm(ci, t0, nt):
+            base = 2 * (ci % 2)
+            isl = slice(t0, t0 + nt)
+            nc.vector.tensor_reduce(out=ms[:, isl], in_=ss_ps[:, base:base + nt, :], axis=AX.X, op=ALU.add)
+            rsqrt(isl)
+
+        o_tiles = {}
+
+        def rope(i, r, q, v_k):
+            bt = ps_t.tile([P, 4, J, 2], F32, name="bt", tag="tp")
+            for hh in range(4):
+                nc.tensor.transpose(bt[:, hh, :, :].rearrange("p j e -> p (j e)"), v_k[:, 4 * q + hh, r * P:(r + 1) * P], ident[:])
+            if q == 0:
+                o_new = epi.tile([P, H, J, 2], F32, name="o")
+                o_tiles[i] = o_new
+            o = o_tiles[i]
+            t1 = epi.tile([P, 4, J, 2], F32, name="t1")
+            t2 = epi.tile([P, 4, J, 2], F32, name="t2")
+            js = slice(i * J, (i + 1) * J)
+            nc.vector.scalar_tensor_tensor(out=t1[:], in0=bt[:], scalar=rstd[:, i:i + 1], in1=cdup[:, js, :].unsqueeze(1).to_broadcast([P, 4, J, 2]), op0=ALU.mult, op1=ALU.mult)
+            nc.vector.scalar_tensor_tensor(out=t2[:], in0=bt[:, :, :, ::-1], scalar=rstd[:, i:i + 1], in1=s3[:, js, :].unsqueeze(1).to_broadcast([P, 4, J, 2]), op0=ALU.mult, op1=ALU.mult)
+            nc.gpsimd.tensor_tensor(out=o[:, 4 * q:4 * q + 4, :, :], in0=t1[:], in1=t2[:], op=ALU.add)
+            if i == TT - 1:
+                nc.sync.dma_start(out=out_rows[i * P:(i + 1) * P, q * NCH:(q + 1) * NCH], in_=o[:, 4 * q:4 * q + 4, :, :].rearrange("p h j e -> p (h j e)"))
+            elif q == 2:
+                nc.sync.dma_start(out=out_rows[i * P:(i + 1) * P, :], in_=o[:].rearrange("p h j e -> p (h j e)"))
+
+        with tc.manual_schedule(engines={mybir.EngineType.PE}):
+            x_front(0)
+            t0, nt = CHUNKS[0]
+            v_k = vpool.tile([P, H, nt * P], F32, name="v")
+            sq_k = sqp.tile([P, H, nt * P], F32, name="sq")
+            units = [(h0, nh, gg) for (h0, nh) in W_BLOCKS for gg in range(G)]
+            held = None
+            for (h0, nh, gg) in units:
+                wg = w_copy(h0, nh, gg)
+                if held is not None:
+                    w_quant(held[0], held[1], held[2], held[3])
+                    if held[2] == G - 1:
+                        for hp in range(held[0] // 2, (held[0] + held[1]) // 2):
+                            acc = mx(t0, nt, hp)
+                            ev(hp, acc, v_k, sq_k, True)
+                        if held[0] == 0:
+                            x_front(1)
+                        if held[0] == 4:
+                            ssq(nt, sq_k, list(range(0, 4)), 0)
+                            x_front(2)
+                        if held[0] == 8:
+                            ssq(nt, sq_k, list(range(4, 8)), 0)
+                            x_front(3)
+                held = (h0, nh, gg, wg)
+            w_quant(held[0], held[1], held[2], held[3])
+            ssq(nt, sq_k, list(range(8, 10)), 0)
+            for hp in range(held[0] // 2, (held[0] + held[1]) // 2):
+                acc = mx(t0, nt, hp)
+                ev(hp, acc, v_k, sq_k, True)
+            ssq(nt, sq_k, list(range(10, 12)), 0)
+            norm(0, t0, nt)
+            prev = (t0, nt, v_k, sq_k)
+
+            for ci in range(1, len(CHUNKS) + 1):
+                cur = None
+                if ci < len(CHUNKS):
+                    t0, nt = CHUNKS[ci]
+                    v_k = vpool.tile([P, H, nt * P], F32, name="v")
+                    sq_k = sqp.tile([P, H, nt * P], F32, name="sq")
+                    cur = (t0, nt, v_k, sq_k)
+                for cb in range(3):
+                    if cur is not None:
+                        for hp in (2 * cb, 2 * cb + 1):
+                            acc = mx(cur[0], cur[1], hp)
+                            ev(hp, acc, cur[2], cur[3], False)
+                    if prev is not None:
+                        if cb == 0 and ci > 1:
+                            if prev[1] == 2:
+                                ssq(prev[1], prev[3], list(range(H)), 2 * ((ci - 1) % 2))
+                            else:
+                                ssq(prev[1], prev[3], list(range(8, 12)), 2 * ((ci - 1) % 2))
+                            norm(ci - 1, prev[0], prev[1])
+                        for bank in range(cb * prev[1], (cb + 1) * prev[1]):
+                            rope(prev[0] + bank // 3, bank // 3, bank % 3, prev[2])
+                    if cur is not None and cur[1] == 1 and cb > 0:
+                        ssq(cur[1], cur[3], list(range(4 * cb - 4, 4 * cb)), 2 * (ci % 2))
+                prev = cur

@@ -81,7 +81,7 @@ def tile_causalwanmodel_pa_kernel(tc, x, w_bytes, w_scale, b, g, freqs_cos, freq
         eps_t = keep.tile([P, 1], F32, name="eps_t")
         nc.vector.memset(eps_t[:], EPS)
         warm = keep.tile([P, 1], F32, name="warm")
-        nc.scalar.activation(out=warm[:], in_=sgn[:, 1:2], func=ACT.Sqrt)
+        nc.scalar.activation(out=warm[:], in_=sgn[:, 1:2], func=ACT.Abs_reciprocal_sqrt)
         ident = keep.tile([P, P], F32, name="ident")
         make_identity(nc, ident[:])
 
@@ -168,15 +168,13 @@ def tile_causalwanmodel_pa_kernel(tc, x, w_bytes, w_scale, b, g, freqs_cos, freq
                 for h in heads:
                     nc.tensor.matmul(out=ss_ps[:, base + r, :], lhsT=sq_k[:, h, r * P:(r + 1) * P], rhs=ident[:], is_transpose=True, start=(h == 0), stop=(h == H - 1))
 
-        def rsqrt(isl):
-            nc.scalar.activation(out=ms[:, isl], in_=ms[:, isl], func=ACT.Sqrt, scale=1.0 / D, bias=eps_t[:])
-            nc.vector.reciprocal(out=rstd[:, isl], in_=ms[:, isl])
-
         def norm(ci, t0, nt):
             base = 2 * (ci % 2)
             isl = slice(t0, t0 + nt)
-            nc.vector.tensor_reduce(out=ms[:, isl], in_=ss_ps[:, base:base + nt, :], axis=AX.X, op=ALU.add)
-            rsqrt(isl)
+            for r in range(nt):
+                junk = epi.tile([P, P], F32, name="junk")
+                nc.scalar.activation(out=junk[:], in_=ss_ps[:, base + r, :], func=ACT.Copy, accum_out=ms[:, t0 + r:t0 + r + 1])
+            nc.scalar.activation(out=rstd[:, isl], in_=ms[:, isl], func=ACT.Abs_reciprocal_sqrt, scale=1.0 / D, bias=eps_t[:])
 
         o_tiles = {}
 
@@ -198,6 +196,27 @@ def tile_causalwanmodel_pa_kernel(tc, x, w_bytes, w_scale, b, g, freqs_cos, freq
                 nc.sync.dma_start(out=out_rows[i * P:(i + 1) * P, q * NCH:(q + 1) * NCH], in_=o[:, 4 * q:4 * q + 4, :, :].rearrange("p h j e -> p (h j e)"))
             elif q == 2:
                 nc.sync.dma_start(out=out_rows[i * P:(i + 1) * P, :], in_=o[:].rearrange("p h j e -> p (h j e)"))
+
+        def rope_unscaled(i, r, q, v_k, add_engine):
+            bt = ps_t.tile([P, 4, J, 2], F32, name="bt", tag="tp")
+            for hh in range(4):
+                nc.tensor.transpose(bt[:, hh, :, :].rearrange("p j e -> p (j e)"), v_k[:, 4 * q + hh, r * P:(r + 1) * P], ident[:])
+            t1 = epi.tile([P, 4, J, 2], F32, name="t1")
+            t2 = epi.tile([P, 4, J, 2], F32, name="t2")
+            un = epi.tile([P, 4, J, 2], F32, name="un")
+            js = slice(i * J, (i + 1) * J)
+            nc.vector.tensor_tensor(out=t1[:], in0=bt[:], in1=cdup[:, js, :].unsqueeze(1).to_broadcast([P, 4, J, 2]), op=ALU.mult)
+            nc.vector.tensor_tensor(out=t2[:], in0=bt[:, :, :, ::-1], in1=s3[:, js, :].unsqueeze(1).to_broadcast([P, 4, J, 2]), op=ALU.mult)
+            add_engine.tensor_tensor(out=un[:], in0=t1[:], in1=t2[:], op=ALU.add)
+            return un
+
+        def scale_store(i, q, un, on_vector):
+            fin = epi.tile([P, 4, J, 2], F32, name="fin")
+            if on_vector:
+                nc.vector.tensor_scalar(out=fin[:], in0=un[:], scalar1=rstd[:, i:i + 1], scalar2=None, op0=ALU.mult)
+            else:
+                nc.scalar.activation(out=fin[:], in_=un[:], func=ACT.Copy, scale=rstd[:, i:i + 1])
+            nc.sync.dma_start(out=out_rows[i * P:(i + 1) * P, q * NCH:(q + 1) * NCH], in_=fin[:].rearrange("p h j e -> p (h j e)"))
 
         with tc.manual_schedule(engines={mybir.EngineType.PE}):
             x_front(0)
@@ -232,7 +251,8 @@ def tile_causalwanmodel_pa_kernel(tc, x, w_bytes, w_scale, b, g, freqs_cos, freq
             norm(0, t0, nt)
             prev = (t0, nt, v_k, sq_k)
 
-            for ci in range(1, len(CHUNKS) + 1):
+            late = []
+            for ci in range(1, len(CHUNKS)):
                 cur = None
                 if ci < len(CHUNKS):
                     t0, nt = CHUNKS[ci]
@@ -255,4 +275,14 @@ def tile_causalwanmodel_pa_kernel(tc, x, w_bytes, w_scale, b, g, freqs_cos, freq
                             rope(prev[0] + bank // 3, bank // 3, bank % 3, prev[2])
                     if cur is not None and cur[1] == 1 and cb > 0:
                         ssq(cur[1], cur[3], list(range(4 * cb - 4, 4 * cb)), 2 * (ci % 2))
+                        if ci == len(CHUNKS) - 1:
+                            late.append(rope_unscaled(cur[0], 0, cb - 1, cur[2], nc.gpsimd))
                 prev = cur
+
+            ci = len(CHUNKS)
+            late.append(rope_unscaled(prev[0], 0, 2, prev[2], nc.vector))
+            ssq(prev[1], prev[3], list(range(8, 12)), 2 * ((ci - 1) % 2))
+            norm(ci - 1, prev[0], prev[1])
+            scale_store(prev[0], 0, late[0], False)
+            scale_store(prev[0], 2, late[2], True)
+            scale_store(prev[0], 1, late[1], False)

@@ -26,7 +26,7 @@ TT = T // P
 XU = 256
 EPS = 1e-6
 FLOPS = 2 * T * D * D
-CHUNKS = ((0, 1), (1, 2), (3, 2), (5, 2), (7, 1))
+CHUNKS = ((0, 1), (1, 2), (3, 2), (5, 1), (6, 1), (7, 1))
 W_BLOCKS = ((0, 4), (4, 4), (8, 2), (10, 2))
 
 
@@ -218,6 +218,11 @@ def tile_causalwanmodel_pa_kernel(tc, x, w_bytes, w_scale, b, g, freqs_cos, freq
                 nc.scalar.activation(out=fin[:], in_=un[:], func=ACT.Copy, scale=rstd[:, i:i + 1])
             nc.sync.dma_start(out=out_rows[i * P:(i + 1) * P, q * NCH:(q + 1) * NCH], in_=fin[:].rearrange("p h j e -> p (h j e)"))
 
+        def warm_up(n):
+            dummy = ps_t.tile([P, NCH], F32, name="dummy", tag="tp")
+            for rep in range(n):
+                nc.tensor.matmul(out=dummy[:], lhsT=bg_rows[:], rhs=x_sb[:, 0, 0:NCH], start=True, stop=True)
+
         with tc.manual_schedule(engines={mybir.EngineType.PE}):
             x_front(0)
             t0, nt = CHUNKS[0]
@@ -241,6 +246,7 @@ def tile_causalwanmodel_pa_kernel(tc, x, w_bytes, w_scale, b, g, freqs_cos, freq
                         if held[0] == 8:
                             ssq(nt, sq_k, list(range(4, 8)), 0)
                             x_front(3)
+                            warm_up(6)
                 held = (h0, nh, gg, wg)
             w_quant(held[0], held[1], held[2], held[3])
             ssq(nt, sq_k, list(range(8, 10)), 0)

@@ -163,15 +163,15 @@ def tile_causalwanmodel_pa_kernel(tc, x, w_bytes, w_scale, b, g, freqs_cos, freq
                 else:
                     nc.scalar.activation(out=v_k[:, h, :], in_=acc[:, a, :], func=ACT.Identity, scale=bgc[:, 32 + h:33 + h], bias=gb[:, h:h + 1])
 
-        def ssq(nt, sq_k, heads, base):
-            for r in range(nt):
+        def ssq(nt, sq_k, heads, base, first=0):
+            for r in range(first, nt):
                 for h in heads:
                     nc.tensor.matmul(out=ss_ps[:, base + r, :], lhsT=sq_k[:, h, r * P:(r + 1) * P], rhs=ident[:], is_transpose=True, start=(h == 0), stop=(h == H - 1))
 
-        def norm(ci, t0, nt):
+        def norm(ci, t0, nt, first=0):
             base = 2 * (ci % 2)
-            isl = slice(t0, t0 + nt)
-            for r in range(nt):
+            isl = slice(t0 + first, t0 + nt)
+            for r in range(first, nt):
                 junk = epi.tile([P, P], F32, name="junk")
                 nc.scalar.activation(out=junk[:], in_=ss_ps[:, base + r, :], func=ACT.Copy, accum_out=ms[:, t0 + r:t0 + r + 1])
             nc.scalar.activation(out=rstd[:, isl], in_=ms[:, isl], func=ACT.Abs_reciprocal_sqrt, scale=1.0 / D, bias=eps_t[:])
@@ -273,11 +273,17 @@ def tile_causalwanmodel_pa_kernel(tc, x, w_bytes, w_scale, b, g, freqs_cos, freq
                     if prev is not None:
                         if cb == 0 and ci > 1:
                             if prev[1] == 2:
-                                ssq(prev[1], prev[3], list(range(H)), 2 * ((ci - 1) % 2))
+                                ssq(1, prev[3], list(range(H)), 2 * ((ci - 1) % 2))
                             else:
-                                ssq(prev[1], prev[3], list(range(8, 12)), 2 * ((ci - 1) % 2))
-                            norm(ci - 1, prev[0], prev[1])
-                        for bank in range(cb * prev[1], (cb + 1) * prev[1]):
+                                ssq(1, prev[3], list(range(8, 12)), 2 * ((ci - 1) % 2))
+                            norm(ci - 1, prev[0], 1)
+                        if cb == 1 and ci > 1 and prev[1] == 2:
+                            ssq(2, prev[3], list(range(H)), 2 * ((ci - 1) % 2), 1)
+                            norm(ci - 1, prev[0], 2, 1)
+                        banks = range(cb * prev[1], (cb + 1) * prev[1])
+                        if ci == len(CHUNKS) - 1:
+                            banks = ((0, 1), (2,), ())[cb]
+                        for bank in banks:
                             rope(prev[0] + bank // 3, bank // 3, bank % 3, prev[2])
                     if cur is not None and cur[1] == 1 and cb > 0:
                         ssq(cur[1], cur[3], list(range(4 * cb - 4, 4 * cb)), 2 * (ci % 2))

@@ -197,10 +197,24 @@ def tile_causalwanmodel_pa_kernel(tc, x, w_bytes, w_scale, b, g, freqs_cos, freq
             elif q == 2:
                 nc.sync.dma_start(out=out_rows[i * P:(i + 1) * P, :], in_=o[:].rearrange("p h j e -> p (h j e)"))
 
-        def rope_unscaled(i, r, q, v_k, add_engine):
+        def bank_back(r, q, v_k):
             bt = ps_t.tile([P, 4, J, 2], F32, name="bt", tag="tp")
             for hh in range(4):
                 nc.tensor.transpose(bt[:, hh, :, :].rearrange("p j e -> p (j e)"), v_k[:, 4 * q + hh, r * P:(r + 1) * P], ident[:])
+            return bt
+
+        def rope_store(i, q, bt, add_engine):
+            t1 = epi.tile([P, 4, J, 2], F32, name="t1")
+            t2 = epi.tile([P, 4, J, 2], F32, name="t2")
+            fin = epi.tile([P, 4, J, 2], F32, name="fin")
+            js = slice(i * J, (i + 1) * J)
+            nc.vector.scalar_tensor_tensor(out=t1[:], in0=bt[:], scalar=rstd[:, i:i + 1], in1=cdup[:, js, :].unsqueeze(1).to_broadcast([P, 4, J, 2]), op0=ALU.mult, op1=ALU.mult)
+            nc.vector.scalar_tensor_tensor(out=t2[:], in0=bt[:, :, :, ::-1], scalar=rstd[:, i:i + 1], in1=s3[:, js, :].unsqueeze(1).to_broadcast([P, 4, J, 2]), op0=ALU.mult, op1=ALU.mult)
+            add_engine.tensor_tensor(out=fin[:], in0=t1[:], in1=t2[:], op=ALU.add)
+            nc.sync.dma_start(out=out_rows[i * P:(i + 1) * P, q * NCH:(q + 1) * NCH], in_=fin[:].rearrange("p h j e -> p (h j e)"))
+
+        def rope_unscaled(i, r, q, v_k, add_engine):
+            bt = bank_back(r, q, v_k)
             t1 = epi.tile([P, 4, J, 2], F32, name="t1")
             t2 = epi.tile([P, 4, J, 2], F32, name="t2")
             un = epi.tile([P, 4, J, 2], F32, name="un")
@@ -280,21 +294,19 @@ def tile_causalwanmodel_pa_kernel(tc, x, w_bytes, w_scale, b, g, freqs_cos, freq
                         if cb == 1 and ci > 1 and prev[1] == 2:
                             ssq(2, prev[3], list(range(H)), 2 * ((ci - 1) % 2), 1)
                             norm(ci - 1, prev[0], 2, 1)
-                        banks = range(cb * prev[1], (cb + 1) * prev[1])
-                        if ci == len(CHUNKS) - 1:
-                            banks = ((0, 1), (2,), ())[cb]
+                        banks = (((0, 1), (2,), ()), ((0, 1, 2), (3, 4), (5,)))[prev[1] - 1][cb]
                         for bank in banks:
                             rope(prev[0] + bank // 3, bank // 3, bank % 3, prev[2])
                     if cur is not None and cur[1] == 1 and cb > 0:
                         ssq(cur[1], cur[3], list(range(4 * cb - 4, 4 * cb)), 2 * (ci % 2))
                         if ci == len(CHUNKS) - 1:
-                            late.append(rope_unscaled(cur[0], 0, cb - 1, cur[2], nc.gpsimd))
+                            late.append(rope_unscaled(cur[0], 0, 0, cur[2], nc.gpsimd) if cb == 1 else bank_back(0, 1, cur[2]))
                 prev = cur
 
             ci = len(CHUNKS)
-            late.append(rope_unscaled(prev[0], 0, 2, prev[2], nc.vector))
+            late.append(bank_back(0, 2, prev[2]))
             ssq(prev[1], prev[3], list(range(8, 12)), 2 * ((ci - 1) % 2))
             norm(ci - 1, prev[0], prev[1])
             scale_store(prev[0], 0, late[0], False)
-            scale_store(prev[0], 2, late[2], True)
-            scale_store(prev[0], 1, late[1], False)
+            rope_store(prev[0], 1, late[1], nc.gpsimd)
+            rope_store(prev[0], 2, late[2], nc.vector)

@@ -26,7 +26,7 @@ TT = T // P
 XU = 256
 EPS = 1e-6
 FLOPS = 2 * T * D * D
-CHUNKS = ((0, 1), (1, 2), (3, 2), (5, 1), (6, 1), (7, 1))
+CHUNKS = ((0, 2), (2, 2), (4, 2), (6, 1), (7, 1))
 W_BLOCKS = ((0, 4), (4, 4), (8, 2), (10, 2))
 
 
@@ -39,6 +39,7 @@ def tile_causalwanmodel_pa_kernel(tc, x, w_bytes, w_scale, b, g, freqs_cos, freq
     with ExitStack() as ctx:
         keep = ctx.enter_context(tc.tile_pool(name="keep", bufs=1))
         stage = ctx.enter_context(tc.tile_pool(name="stage", bufs=3))
+        xst = ctx.enter_context(tc.tile_pool(name="xst", bufs=6))
         vpool = ctx.enter_context(tc.tile_pool(name="vpool", bufs=3))
         sqp = ctx.enter_context(tc.tile_pool(name="sqp", bufs=2))
         epi = ctx.enter_context(tc.tile_pool(name="epi", bufs=3))
@@ -48,32 +49,35 @@ def tile_causalwanmodel_pa_kernel(tc, x, w_bytes, w_scale, b, g, freqs_cos, freq
 
         cos_sb = keep.tile([P, TT, J], BF16, name="cos_sb")
         sin_sb = keep.tile([P, TT, J], BF16, name="sin_sb")
-        nc.scalar.dma_start(out=cos_sb[:], in_=freqs_cos.rearrange("(i p) j -> p i j", p=P))
-        nc.scalar.dma_start(out=sin_sb[:], in_=freqs_sin.rearrange("(i p) j -> p i j", p=P))
         bg_rows = keep.tile([P, P], BF16, name="bg_rows")
         nc.vector.memset(bg_rows[:], 0.0)
-        nc.scalar.dma_start(out=bg_rows[0:H, :], in_=b.rearrange("(h p) -> h p", p=P))
-        nc.scalar.dma_start(out=bg_rows[32:32 + H, :], in_=g.rearrange("(h p) -> h p", p=P))
 
         wsc = keep.tile([P, G, PACK], F32, name="wsc")
-        nc.sync.dma_start(out=wsc[:], in_=w_scale.rearrange("(g p t) o -> p g (t o)", p=P, t=PACK))
+        nc.scalar.dma_start(out=wsc[:], in_=w_scale.rearrange("(g p t) o -> p g (t o)", p=P, t=PACK))
         wb = keep.tile([P, G, PACK, D], U8, name="w_bytes_sb")
         x_sb = keep.tile([P, TT, D], BF16, name="x_sb")
 
-        def load_w(c):
-            for gg in range(G):
+        def load_w(c, passes=range(G)):
+            for gg in passes:
                 nc.sync.dma_start(out=wb[:, gg, :, c * NCH:(c + 1) * NCH], in_=w_view[gg][:, :, c * NCH:(c + 1) * NCH])
 
         def load_x(i):
             nc.sync.dma_start(out=x_sb[:, i, :], in_=x_rows[i * P:(i + 1) * P, :])
 
-        load_w(0)
+        load_w(0, (0, 1))
         load_x(0)
         load_x(1)
+        load_w(0, (2,))
+        nc.sync.dma_start(out=bg_rows[0:H, :], in_=b.rearrange("(h p) -> h p", p=P))
+        nc.sync.dma_start(out=bg_rows[32:32 + H, :], in_=g.rearrange("(h p) -> h p", p=P))
         load_w(1)
+        load_x(2)
+        load_x(3)
         load_w(2)
-        for i in range(2, TT):
+        for i in range(4, TT):
             load_x(i)
+        nc.sync.dma_start(out=cos_sb[:], in_=freqs_cos.rearrange("(i p) j -> p i j", p=P))
+        nc.sync.dma_start(out=sin_sb[:], in_=freqs_sin.rearrange("(i p) j -> p i j", p=P))
 
         sgn = keep.tile([P, 2], F32, name="sgn")
         nc.vector.memset(sgn[:, 0:1], -1.0)
@@ -87,47 +91,59 @@ def tile_causalwanmodel_pa_kernel(tc, x, w_bytes, w_scale, b, g, freqs_cos, freq
 
         cdup = keep.tile([P, TT * J, 2], F32, name="cdup")
         s3 = keep.tile([P, TT * J, 2], F32, name="s3")
-        nc.vector.tensor_copy(out=cdup[:], in_=cos_sb[:].rearrange("p i j -> p (i j)").unsqueeze(2).to_broadcast([P, TT * J, 2]))
-        nc.vector.tensor_tensor(
-            out=s3[:], in0=sin_sb[:].rearrange("p i j -> p (i j)").unsqueeze(2).to_broadcast([P, TT * J, 2]),
-            in1=sgn[:].unsqueeze(1).to_broadcast([P, TT * J, 2]), op=ALU.mult,
-        )
+
+        def tables():
+            nc.vector.tensor_copy(out=cdup[:], in_=cos_sb[:].rearrange("p i j -> p (i j)").unsqueeze(2).to_broadcast([P, TT * J, 2]))
+            nc.vector.tensor_tensor(
+                out=s3[:], in0=sin_sb[:].rearrange("p i j -> p (i j)").unsqueeze(2).to_broadcast([P, TT * J, 2]),
+                in1=sgn[:].unsqueeze(1).to_broadcast([P, TT * J, 2]), op=ALU.mult,
+            )
 
         bg_f = keep.tile([P, P], F32, name="bg_f")
-        nc.vector.tensor_copy(out=bg_f[:], in_=bg_rows[:])
-        bg_ps = ps_t.tile([P, P], F32, name="bg_ps", tag="tp")
-        nc.tensor.transpose(bg_ps[:], bg_f[:], ident[:])
         bgc = keep.tile([P, P], F32, name="bgc")
-        nc.vector.tensor_copy(out=bgc[:], in_=bg_ps[:])
         gb = keep.tile([P, H], F32, name="gb")
-        nc.vector.tensor_tensor(out=gb[:], in0=bgc[:, 0:H], in1=bgc[:, 32:32 + H], op=ALU.mult)
+
+        def bias_and_gain():
+            nc.vector.tensor_copy(out=bg_f[:], in_=bg_rows[:])
+            bg_ps = ps_t.tile([P, P], F32, name="bg_ps", tag="tp")
+            nc.tensor.transpose(bg_ps[:], bg_f[:], ident[:])
+            nc.vector.tensor_copy(out=bgc[:], in_=bg_ps[:])
+            nc.vector.tensor_tensor(out=gb[:], in0=bgc[:, 0:H], in1=bgc[:, 32:32 + H], op=ALU.mult)
 
         w_codes = keep.tile([P, G, D], U32, name="w_codes", align_bytes=64)
         w_scl = keep.tile([P, G, D], U8, name="w_scl", align_bytes=64)
         x_codes = keep.tile([P, G, T], U32, name="x_codes", align_bytes=64)
         x_scl = keep.tile([P, G, T], U8, name="x_scl", align_bytes=64)
 
-        def x_front(xu):
-            xs = slice(xu * XU, (xu + 1) * XU)
-            for gg in range(G):
-                xt = ps_t.tile([P, 2, XU], F32, name="xt", tag="tp")
-                for r in range(2):
-                    words = x_sb[:, 2 * xu + r, :].bitcast(F32)
-                    for u in range(2):
-                        nc.tensor.transpose(xt[:, u, r * P:(r + 1) * P], words[:, 256 * gg + u:256 * (gg + 1):2], ident[:])
-                xg = stage.tile([P, XU * PACK], BF16, name="xg", align_bytes=64)
-                nc.scalar.copy(out=xg[:].bitcast(F32).rearrange("p (r u) -> p r u", u=2), in_=xt[:].rearrange("p u r -> p r u"))
-                nc.vector.quantize_mx(out=x_codes[:, gg, xs].bitcast(FP8X4), scales=x_scl[:, gg, xs], in_=xg[:])
+        def x_turn(xu, gg):
+            xt = ps_t.tile([P, 2, XU], F32, name="xt", tag="tp")
+            for r in range(2):
+                words = x_sb[:, 2 * xu + r, :].bitcast(F32)
+                for u in range(2):
+                    nc.tensor.transpose(xt[:, u, r * P:(r + 1) * P], words[:, 256 * gg + u:256 * (gg + 1):2], ident[:])
+            return xt
 
-        def w_copy(h0, nh, gg):
+        def x_copy(xt):
+            xg = xst.tile([P, XU * PACK], BF16, name="xg", align_bytes=64)
+            nc.scalar.copy(out=xg[:].bitcast(F32).rearrange("p (r u) -> p r u", u=2), in_=xt[:].rearrange("p u r -> p r u"))
+            return xg
+
+        def x_quant(xu, gg, xg):
+            xs = slice(xu * XU, (xu + 1) * XU)
+            nc.vector.quantize_mx(out=x_codes[:, gg, xs].bitcast(FP8X4), scales=x_scl[:, gg, xs], in_=xg[:])
+
+        def w_widen(h0, nh, gg, on_vector=1):
             cs = slice(h0 * P, (h0 + nh) * P)
             wide = stage.tile([P, PACK, nh * P], BF16, name="wide")
             for t in range(PACK):
                 src = wb[:, gg, t, cs].bitcast(FP8)
-                if t == 3:
+                if t >= PACK - on_vector:
                     nc.vector.tensor_scalar(out=wide[:, t, :], in0=src, scalar1=wsc[:, gg, t:t + 1], scalar2=None, op0=ALU.mult)
                 else:
                     nc.scalar.activation(out=wide[:, t, :], in_=src, func=ACT.Copy, scale=wsc[:, gg, t:t + 1])
+            return wide
+
+        def w_mix(nh, wide):
             wg = stage.tile([P, nh * P, PACK], BF16, name="wg", align_bytes=64)
             nc.vector.tensor_copy(out=wg[:].rearrange("p (c i) t -> p c t i", i=4), in_=wide[:].rearrange("p t (c i) -> p c t i", i=4))
             return wg
@@ -158,7 +174,9 @@ def tile_causalwanmodel_pa_kernel(tc, x, w_bytes, w_scale, b, g, freqs_cos, freq
             for a in range(2):
                 h = 2 * hp + a
                 nc.scalar.activation(out=sq_k[:, h, :], in_=acc[:, a, :], func=ACT.Square, bias=bgc[:, h:h + 1])
-                if v_on_vector and h % 3 == 0:
+            for a in range(2):
+                h = 2 * hp + a
+                if v_on_vector:
                     nc.vector.tensor_scalar(out=v_k[:, h, :], in0=acc[:, a, :], scalar1=bgc[:, 32 + h:33 + h], scalar2=gb[:, h:h + 1], op0=ALU.mult, op1=ALU.add)
                 else:
                     nc.scalar.activation(out=v_k[:, h, :], in_=acc[:, a, :], func=ACT.Identity, scale=bgc[:, 32 + h:33 + h], bias=gb[:, h:h + 1])
@@ -237,72 +255,102 @@ def tile_causalwanmodel_pa_kernel(tc, x, w_bytes, w_scale, b, g, freqs_cos, freq
             for rep in range(n):
                 nc.tensor.matmul(out=dummy[:], lhsT=bg_rows[:], rhs=x_sb[:, 0, 0:NCH], start=True, stop=True)
 
-        with tc.manual_schedule(engines={mybir.EngineType.PE}):
-            x_front(0)
-            t0, nt = CHUNKS[0]
-            v_k = vpool.tile([P, H, nt * P], F32, name="v")
-            sq_k = sqp.tile([P, H, nt * P], F32, name="sq")
+        V0 = [0,2]
+        V1 = []
+        EX = {12: ((1, 0),), 13: ((1, 1),)}
+        with tc.manual_schedule():
             units = [(h0, nh, gg) for (h0, nh) in W_BLOCKS for gg in range(G)]
-            held = None
-            for (h0, nh, gg) in units:
-                wg = w_copy(h0, nh, gg)
-                if held is not None:
-                    w_quant(held[0], held[1], held[2], held[3])
-                    if held[2] == G - 1:
-                        for hp in range(held[0] // 2, (held[0] + held[1]) // 2):
-                            acc = mx(t0, nt, hp)
-                            ev(hp, acc, v_k, sq_k, True)
-                        if held[0] == 0:
-                            x_front(1)
-                        if held[0] == 4:
-                            ssq(nt, sq_k, list(range(0, 4)), 0)
-                            x_front(2)
-                        if held[0] == 8:
-                            ssq(nt, sq_k, list(range(4, 8)), 0)
-                            x_front(3)
-                            warm_up(6)
-                held = (h0, nh, gg, wg)
-            w_quant(held[0], held[1], held[2], held[3])
-            ssq(nt, sq_k, list(range(8, 10)), 0)
-            for hp in range(held[0] // 2, (held[0] + held[1]) // 2):
-                acc = mx(t0, nt, hp)
-                ev(hp, acc, v_k, sq_k, True)
-            ssq(nt, sq_k, list(range(10, 12)), 0)
-            norm(0, t0, nt)
-            prev = (t0, nt, v_k, sq_k)
-
+            xjobs = {0: ((0, 0), (0, 1)), 1: ((0, 2),), 3: ((1, 0),), 4: ((1, 1),), 5: ((1, 2),), 6: ((2, 0),), 8: ((2, 1),), 10: ((2, 2),), 11: ((3, 0), (3, 1), (3, 2))}
+            vs = {}
+            def chunk(ci):
+                if ci not in vs:
+                    nt_ = CHUNKS[ci][1]
+                    v_new = vpool.tile([P, H, nt_ * P], F32, name="v")
+                    sq_new = sqp.tile([P, H, nt_ * P], F32, name="sq")
+                    vs[ci] = (CHUNKS[ci][0], nt_, v_new, sq_new)
+                return vs[ci]
+            def domx(ci, hp):
+                t0_, nt_, v_, sq_ = chunk(ci)
+                return (ci, hp, mx(t0_, nt_, hp))
+            def doev(ci, hp, acc):
+                t0_, nt_, v_, sq_ = chunk(ci)
+                ev(hp, acc, v_, sq_, (ci == 0 and hp in V0) or (ci == 1 and hp in V1))
+            done = set()
+            prev_w = None
+            turned = []
+            copied = []
+            late_x = []
+            pend = []
+            evd = []
+            n1 = len(units)
+            for i in range(n1 + 2):
+                cur_w = None
+                if i < n1:
+                    h0, nh, gg = units[i]
+                    cur_w = (h0, nh, gg, w_widen(h0, nh, gg, 2 if i == 0 else 1))
+                new_t = [(xu, gg, x_turn(xu, gg)) for (xu, gg) in xjobs.get(i, ())]
+                new_c = [(xu, gg, x_copy(xt)) for (xu, gg, xt) in turned]
+                if i == 3:
+                    bias_and_gain()
+                if evd:
+                    ssq(1, chunk(0)[3], evd, 0)
+                    evd = []
+                if prev_w is not None:
+                    w_quant(prev_w[0], prev_w[1], prev_w[2], prev_w[3])
+                for xi in copied:
+                    if xi[0] < 2:
+                        x_quant(*xi)
+                    else:
+                        late_x.append(xi)
+                if cur_w is not None:
+                    wg = w_mix(cur_w[1], cur_w[3])
+                for (ci, hp, acc) in pend:
+                    doev(ci, hp, acc)
+                    done.add((ci, hp))
+                    if ci == 0:
+                        evd = evd + [2 * hp, 2 * hp + 1]
+                pend = []
+                if prev_w is not None and prev_w[2] == G - 1:
+                    h0, nh = prev_w[0], prev_w[1]
+                    pend = [domx(0, hp) for hp in range(h0 // 2, (h0 + nh) // 2)]
+                for (ci, hp) in EX.get(i, ()):
+                    pend.append(domx(ci, hp))
+                prev_w = (cur_w[0], cur_w[1], cur_w[2], wg) if cur_w is not None else None
+                turned = new_t
+                copied = new_c
+            ssq(1, chunk(0)[3], evd, 0)
+            norm(0, 0, 1)
+            for (ci, hp, acc) in pend:
+                doev(ci, hp, acc)
+                done.add((ci, hp))
+            for xi in late_x + copied:
+                x_quant(*xi)
+            tables()
+            prev = chunk(0)
             late = []
             for ci in range(1, len(CHUNKS)):
-                cur = None
-                if ci < len(CHUNKS):
-                    t0, nt = CHUNKS[ci]
-                    v_k = vpool.tile([P, H, nt * P], F32, name="v")
-                    sq_k = sqp.tile([P, H, nt * P], F32, name="sq")
-                    cur = (t0, nt, v_k, sq_k)
+                cur = chunk(ci)
                 for cb in range(3):
-                    if cur is not None:
-                        for hp in (2 * cb, 2 * cb + 1):
-                            acc = mx(cur[0], cur[1], hp)
-                            ev(hp, acc, cur[2], cur[3], False)
-                    if prev is not None:
-                        if cb == 0 and ci > 1:
-                            if prev[1] == 2:
-                                ssq(1, prev[3], list(range(H)), 2 * ((ci - 1) % 2))
-                            else:
-                                ssq(1, prev[3], list(range(8, 12)), 2 * ((ci - 1) % 2))
-                            norm(ci - 1, prev[0], 1)
-                        if cb == 1 and ci > 1 and prev[1] == 2:
-                            ssq(2, prev[3], list(range(H)), 2 * ((ci - 1) % 2), 1)
-                            norm(ci - 1, prev[0], 2, 1)
-                        banks = (((0, 1), (2,), ()), ((0, 1, 2), (3, 4), (5,)))[prev[1] - 1][cb]
-                        for bank in banks:
-                            rope(prev[0] + bank // 3, bank // 3, bank % 3, prev[2])
-                    if cur is not None and cur[1] == 1 and cb > 0:
+                    for hp in (2 * cb, 2 * cb + 1):
+                        if (ci, hp) not in done:
+                            doev(*domx(ci, hp))
+                    if cb == 0 and ci > 1:
+                        if prev[1] == 2:
+                            ssq(1, prev[3], list(range(H)), 2 * ((ci - 1) % 2))
+                        else:
+                            ssq(1, prev[3], list(range(8, 12)), 2 * ((ci - 1) % 2))
+                        norm(ci - 1, prev[0], 1)
+                    if cb == 1 and prev[1] == 2:
+                        ssq(2, prev[3], list(range(H)), 2 * ((ci - 1) % 2), 1)
+                        norm(ci - 1, prev[0], 2, 1)
+                    banks = (((0, 1), (2,), ()), ((0, 1), (2, 3), (4, 5)))[prev[1] - 1][cb]
+                    for bank in banks:
+                        rope(prev[0] + bank // 3, bank // 3, bank % 3, prev[2])
+                    if cur[1] == 1 and cb > 0:
                         ssq(cur[1], cur[3], list(range(4 * cb - 4, 4 * cb)), 2 * (ci % 2))
                         if ci == len(CHUNKS) - 1:
                             late.append(rope_unscaled(cur[0], 0, 0, cur[2], nc.gpsimd) if cb == 1 else bank_back(0, 1, cur[2]))
                 prev = cur
-
             ci = len(CHUNKS)
             late.append(bank_back(0, 2, prev[2]))
             ssq(prev[1], prev[3], list(range(8, 12)), 2 * ((ci - 1) % 2))

@@ -171,9 +171,15 @@ def tile_causalwanmodel_pa_kernel(tc, x, w_bytes, w_scale, b, g, freqs_cos, freq
             return acc
 
         def ev(hp, acc, v_k, sq_k, v_on_vector):
+            ev_sq(hp, acc, sq_k)
+            ev_v(hp, acc, v_k, v_on_vector)
+
+        def ev_sq(hp, acc, sq_k):
             for a in range(2):
                 h = 2 * hp + a
                 nc.scalar.activation(out=sq_k[:, h, :], in_=acc[:, a, :], func=ACT.Square, bias=bgc[:, h:h + 1])
+
+        def ev_v(hp, acc, v_k, v_on_vector):
             for a in range(2):
                 h = 2 * hp + a
                 if v_on_vector:
@@ -185,6 +191,13 @@ def tile_causalwanmodel_pa_kernel(tc, x, w_bytes, w_scale, b, g, freqs_cos, freq
             for r in range(first, nt):
                 for h in heads:
                     nc.tensor.matmul(out=ss_ps[:, base + r, :], lhsT=sq_k[:, h, r * P:(r + 1) * P], rhs=ident[:], is_transpose=True, start=(h == 0), stop=(h == H - 1))
+
+        def norm_v(ci, t0, nt, first=0):
+            base = 2 * (ci % 2)
+            isl = slice(t0 + first, t0 + nt)
+            for r in range(first, nt):
+                nc.vector.tensor_reduce(out=ms[:, t0 + r:t0 + r + 1], in_=ss_ps[:, base + r, :], axis=AX.X, op=ALU.add)
+            nc.scalar.activation(out=rstd[:, isl], in_=ms[:, isl], func=ACT.Abs_reciprocal_sqrt, scale=1.0 / D, bias=eps_t[:])
 
         def norm(ci, t0, nt, first=0):
             base = 2 * (ci % 2)
@@ -253,11 +266,16 @@ def tile_causalwanmodel_pa_kernel(tc, x, w_bytes, w_scale, b, g, freqs_cos, freq
         def warm_up(n):
             dummy = ps_t.tile([P, NCH], F32, name="dummy", tag="tp")
             for rep in range(n):
-                nc.tensor.matmul(out=dummy[:], lhsT=bg_rows[:], rhs=x_sb[:, 0, 0:NCH], start=True, stop=True)
+                nc.tensor.matmul(out=dummy[:], lhsT=x_sb[:, 0, 0:P], rhs=x_sb[:, 0, 0:NCH], start=True, stop=True)
 
         V0 = [0,2]
         V1 = []
-        EX = {12: ((1, 0),), 13: ((1, 1),)}
+        WARM = {3: 4, 6: 4, 9: 4}
+        NV = {}
+        VL = {}
+        def nrm(ci, t0, nt, first=0):
+            (norm_v if (ci, first) in NV else norm)(ci, t0, nt, first)
+        EX = {}
         with tc.manual_schedule():
             units = [(h0, nh, gg) for (h0, nh) in W_BLOCKS for gg in range(G)]
             xjobs = {0: ((0, 0), (0, 1)), 1: ((0, 2),), 3: ((1, 0),), 4: ((1, 1),), 5: ((1, 2),), 6: ((2, 0),), 8: ((2, 1),), 10: ((2, 2),), 11: ((3, 0), (3, 1), (3, 2))}
@@ -283,11 +301,11 @@ def tile_causalwanmodel_pa_kernel(tc, x, w_bytes, w_scale, b, g, freqs_cos, freq
             pend = []
             evd = []
             n1 = len(units)
-            for i in range(n1 + 2):
+            for i in range(n1 + 1):
                 cur_w = None
                 if i < n1:
                     h0, nh, gg = units[i]
-                    cur_w = (h0, nh, gg, w_widen(h0, nh, gg, 2 if i == 0 else 1))
+                    cur_w = (h0, nh, gg, w_widen(h0, nh, gg, {0: 2, 11: 2}.get(i, 1)))
                 new_t = [(xu, gg, x_turn(xu, gg)) for (xu, gg) in xjobs.get(i, ())]
                 new_c = [(xu, gg, x_copy(xt)) for (xu, gg, xt) in turned]
                 if i == 3:
@@ -295,6 +313,8 @@ def tile_causalwanmodel_pa_kernel(tc, x, w_bytes, w_scale, b, g, freqs_cos, freq
                 if evd:
                     ssq(1, chunk(0)[3], evd, 0)
                     evd = []
+                if i in WARM:
+                    warm_up(WARM[i])
                 if prev_w is not None:
                     w_quant(prev_w[0], prev_w[1], prev_w[2], prev_w[3])
                 for xi in copied:
@@ -318,12 +338,25 @@ def tile_causalwanmodel_pa_kernel(tc, x, w_bytes, w_scale, b, g, freqs_cos, freq
                 prev_w = (cur_w[0], cur_w[1], cur_w[2], wg) if cur_w is not None else None
                 turned = new_t
                 copied = new_c
-            ssq(1, chunk(0)[3], evd, 0)
-            norm(0, 0, 1)
+            if evd:
+                ssq(1, chunk(0)[3], evd, 0)
+                evd = []
+            new_c = [(xu, gg, x_copy(xt)) for (xu, gg, xt) in turned]
+            c1 = [domx(1, hp) for hp in (0, 1)]
             for (ci, hp, acc) in pend:
                 doev(ci, hp, acc)
                 done.add((ci, hp))
-            for xi in late_x + copied:
+                if ci == 0:
+                    evd = evd + [2 * hp, 2 * hp + 1]
+            for x3 in c1[0:1]:
+                doev(*x3)
+            ssq(1, chunk(0)[3], evd, 0)
+            nrm(0, 0, 1)
+            for x3 in c1[1:]:
+                doev(*x3)
+            for x3 in c1:
+                done.add((x3[0], x3[1]))
+            for xi in late_x + copied + new_c:
                 x_quant(*xi)
             tables()
             prev = chunk(0)
@@ -331,21 +364,32 @@ def tile_causalwanmodel_pa_kernel(tc, x, w_bytes, w_scale, b, g, freqs_cos, freq
             for ci in range(1, len(CHUNKS)):
                 cur = chunk(ci)
                 for cb in range(3):
-                    for hp in (2 * cb, 2 * cb + 1):
-                        if (ci, hp) not in done:
-                            doev(*domx(ci, hp))
+                    held = []
+                    accs = [domx(ci, hp) for hp in (2 * cb, 2 * cb + 1) if (ci, hp) not in done]
+                    def evx(x3):
+                        if (x3[0], x3[1]) in VL:
+                            ev_sq(x3[1], x3[2], cur[3])
+                            held.append((x3[1], x3[2]))
+                        else:
+                            doev(*x3)
+                    for x3 in accs[0:1]:
+                        evx(x3)
                     if cb == 0 and ci > 1:
                         if prev[1] == 2:
                             ssq(1, prev[3], list(range(H)), 2 * ((ci - 1) % 2))
                         else:
                             ssq(1, prev[3], list(range(8, 12)), 2 * ((ci - 1) % 2))
-                        norm(ci - 1, prev[0], 1)
+                        nrm(ci - 1, prev[0], 1)
                     if cb == 1 and prev[1] == 2:
                         ssq(2, prev[3], list(range(H)), 2 * ((ci - 1) % 2), 1)
-                        norm(ci - 1, prev[0], 2, 1)
+                        nrm(ci - 1, prev[0], 2, 1)
+                    for x3 in accs[1:]:
+                        evx(x3)
                     banks = (((0, 1), (2,), ()), ((0, 1), (2, 3), (4, 5)))[prev[1] - 1][cb]
                     for bank in banks:
                         rope(prev[0] + bank // 3, bank // 3, bank % 3, prev[2])
+                    for (hp, acc_) in held:
+                        ev_v(hp, acc_, cur[2], True)
                     if cur[1] == 1 and cb > 0:
                         ssq(cur[1], cur[3], list(range(4 * cb - 4, 4 * cb)), 2 * (ci % 2))
                         if ci == len(CHUNKS) - 1:

@@ -57,25 +57,25 @@ def tile_causalwanmodel_pa_kernel(tc, x, w_bytes, w_scale, b, g, freqs_cos, freq
         wb = keep.tile([P, G, PACK, D], U8, name="w_bytes_sb")
         x_sb = keep.tile([P, TT, D], BF16, name="x_sb")
 
-        def load_w(c, passes=range(G)):
-            for gg in passes:
-                nc.sync.dma_start(out=wb[:, gg, :, c * NCH:(c + 1) * NCH], in_=w_view[gg][:, :, c * NCH:(c + 1) * NCH])
+        def load_w(gg, cols):
+            nc.sync.dma_start(out=wb[:, gg, :, cols], in_=w_view[gg][:, :, cols])
 
-        def load_x(i):
-            nc.sync.dma_start(out=x_sb[:, i, :], in_=x_rows[i * P:(i + 1) * P, :])
+        def load_x(i, n):
+            nc.sync.dma_start(out=x_sb[:, i:i + n, :], in_=x_rows[i * P:(i + n) * P, :].rearrange("(i p) k -> p i k", p=P))
 
-        load_w(0, (0, 1))
-        load_x(0)
-        load_x(1)
-        load_w(0, (2,))
+        load_w(0, slice(0, NCH))
+        load_w(1, slice(0, NCH))
+        load_x(0, 1)
+        load_x(1, 1)
+        load_w(2, slice(0, NCH))
         nc.sync.dma_start(out=bg_rows[0:H, :], in_=b.rearrange("(h p) -> h p", p=P))
         nc.sync.dma_start(out=bg_rows[32:32 + H, :], in_=g.rearrange("(h p) -> h p", p=P))
-        load_w(1)
-        load_x(2)
-        load_x(3)
-        load_w(2)
-        for i in range(4, TT):
-            load_x(i)
+        load_w(0, slice(NCH, D))
+        load_x(2, 2)
+        load_w(1, slice(NCH, D))
+        load_w(2, slice(NCH, D))
+        for i in range(4, TT, 2):
+            load_x(i, 2)
         nc.sync.dma_start(out=cos_sb[:], in_=freqs_cos.rearrange("(i p) j -> p i j", p=P))
         nc.sync.dma_start(out=sin_sb[:], in_=freqs_sin.rearrange("(i p) j -> p i j", p=P))
 
@@ -92,11 +92,12 @@ def tile_causalwanmodel_pa_kernel(tc, x, w_bytes, w_scale, b, g, freqs_cos, freq
         cdup = keep.tile([P, TT * J, 2], F32, name="cdup")
         s3 = keep.tile([P, TT * J, 2], F32, name="s3")
 
-        def tables():
-            nc.vector.tensor_copy(out=cdup[:], in_=cos_sb[:].rearrange("p i j -> p (i j)").unsqueeze(2).to_broadcast([P, TT * J, 2]))
+        def tables(i0, n):
+            js = slice(i0 * J, (i0 + n) * J)
+            nc.vector.tensor_copy(out=cdup[:, js, :], in_=cos_sb[:].rearrange("p i j -> p (i j)")[:, js].unsqueeze(2).to_broadcast([P, n * J, 2]))
             nc.vector.tensor_tensor(
-                out=s3[:], in0=sin_sb[:].rearrange("p i j -> p (i j)").unsqueeze(2).to_broadcast([P, TT * J, 2]),
-                in1=sgn[:].unsqueeze(1).to_broadcast([P, TT * J, 2]), op=ALU.mult,
+                out=s3[:, js, :], in0=sin_sb[:].rearrange("p i j -> p (i j)")[:, js].unsqueeze(2).to_broadcast([P, n * J, 2]),
+                in1=sgn[:].unsqueeze(1).to_broadcast([P, n * J, 2]), op=ALU.mult,
             )
 
         bg_f = keep.tile([P, P], F32, name="bg_f")
@@ -107,6 +108,9 @@ def tile_causalwanmodel_pa_kernel(tc, x, w_bytes, w_scale, b, g, freqs_cos, freq
             nc.vector.tensor_copy(out=bg_f[:], in_=bg_rows[:])
             bg_ps = ps_t.tile([P, P], F32, name="bg_ps", tag="tp")
             nc.tensor.transpose(bg_ps[:], bg_f[:], ident[:])
+            return bg_ps
+
+        def bias_and_gain2(bg_ps):
             nc.vector.tensor_copy(out=bgc[:], in_=bg_ps[:])
             nc.vector.tensor_tensor(out=gb[:], in0=bgc[:, 0:H], in1=bgc[:, 32:32 + H], op=ALU.mult)
 
@@ -209,7 +213,7 @@ def tile_causalwanmodel_pa_kernel(tc, x, w_bytes, w_scale, b, g, freqs_cos, freq
 
         o_tiles = {}
 
-        def rope(i, r, q, v_k):
+        def rope(i, r, q, v_k, vadd=()):
             bt = ps_t.tile([P, 4, J, 2], F32, name="bt", tag="tp")
             for hh in range(4):
                 nc.tensor.transpose(bt[:, hh, :, :].rearrange("p j e -> p (j e)"), v_k[:, 4 * q + hh, r * P:(r + 1) * P], ident[:])
@@ -222,7 +226,8 @@ def tile_causalwanmodel_pa_kernel(tc, x, w_bytes, w_scale, b, g, freqs_cos, freq
             js = slice(i * J, (i + 1) * J)
             nc.vector.scalar_tensor_tensor(out=t1[:], in0=bt[:], scalar=rstd[:, i:i + 1], in1=cdup[:, js, :].unsqueeze(1).to_broadcast([P, 4, J, 2]), op0=ALU.mult, op1=ALU.mult)
             nc.vector.scalar_tensor_tensor(out=t2[:], in0=bt[:, :, :, ::-1], scalar=rstd[:, i:i + 1], in1=s3[:, js, :].unsqueeze(1).to_broadcast([P, 4, J, 2]), op0=ALU.mult, op1=ALU.mult)
-            nc.gpsimd.tensor_tensor(out=o[:, 4 * q:4 * q + 4, :, :], in0=t1[:], in1=t2[:], op=ALU.add)
+            add_eng = nc.vector if (i, q) in vadd else nc.gpsimd
+            add_eng.tensor_tensor(out=o[:, 4 * q:4 * q + 4, :, :], in0=t1[:], in1=t2[:], op=ALU.add)
             if i == TT - 1:
                 nc.sync.dma_start(out=out_rows[i * P:(i + 1) * P, q * NCH:(q + 1) * NCH], in_=o[:, 4 * q:4 * q + 4, :, :].rearrange("p h j e -> p (h j e)"))
             elif q == 2:
@@ -275,6 +280,7 @@ def tile_causalwanmodel_pa_kernel(tc, x, w_bytes, w_scale, b, g, freqs_cos, freq
         VL = {}
         def nrm(ci, t0, nt, first=0):
             (norm_v if (ci, first) in NV else norm)(ci, t0, nt, first)
+        XL = {}
         EX = {}
         with tc.manual_schedule():
             units = [(h0, nh, gg) for (h0, nh) in W_BLOCKS for gg in range(G)]
@@ -305,11 +311,13 @@ def tile_causalwanmodel_pa_kernel(tc, x, w_bytes, w_scale, b, g, freqs_cos, freq
                 cur_w = None
                 if i < n1:
                     h0, nh, gg = units[i]
-                    cur_w = (h0, nh, gg, w_widen(h0, nh, gg, {0: 2, 11: 2}.get(i, 1)))
+                    cur_w = (h0, nh, gg, w_widen(h0, nh, gg, {0: 3, 2: 2, 5: 2, 8: 2, 11: 2}.get(i, 1)))
                 new_t = [(xu, gg, x_turn(xu, gg)) for (xu, gg) in xjobs.get(i, ())]
                 new_c = [(xu, gg, x_copy(xt)) for (xu, gg, xt) in turned]
+                if i == 2:
+                    bg_ps = bias_and_gain()
                 if i == 3:
-                    bias_and_gain()
+                    bias_and_gain2(bg_ps)
                 if evd:
                     ssq(1, chunk(0)[3], evd, 0)
                     evd = []
@@ -349,47 +357,77 @@ def tile_causalwanmodel_pa_kernel(tc, x, w_bytes, w_scale, b, g, freqs_cos, freq
                 if ci == 0:
                     evd = evd + [2 * hp, 2 * hp + 1]
             for x3 in c1[0:1]:
-                doev(*x3)
+                ev_sq(x3[1], x3[2], chunk(1)[3])
             ssq(1, chunk(0)[3], evd, 0)
             nrm(0, 0, 1)
+            for x3 in c1[0:1]:
+                ev_v(x3[1], x3[2], chunk(1)[2], False)
             for x3 in c1[1:]:
                 doev(*x3)
             for x3 in c1:
                 done.add((x3[0], x3[1]))
-            for xi in late_x + copied + new_c:
+            x_rest = late_x + copied + new_c
+            for xi in [xi for xi in x_rest if xi[0] < 4]:
                 x_quant(*xi)
-            tables()
+            x_rest = [xi for xi in x_rest if xi[0] >= 4]
+            tables(0, 2)
+            for xi in x_rest[0:0]:
+                x_quant(*xi)
+            x_rest = x_rest[0:]
             prev = chunk(0)
             late = []
+            xlate = []
             for ci in range(1, len(CHUNKS)):
                 cur = chunk(ci)
                 for cb in range(3):
                     held = []
-                    accs = [domx(ci, hp) for hp in (2 * cb, 2 * cb + 1) if (ci, hp) not in done]
+                    todo = [hp for hp in (2 * cb, 2 * cb + 1) if (ci, hp) not in done]
+                    split = cb == 0 and ci == 2
+                    accs = [domx(ci, hp) for hp in (todo[0:1] if split else todo)]
                     def evx(x3):
                         if (x3[0], x3[1]) in VL:
                             ev_sq(x3[1], x3[2], cur[3])
                             held.append((x3[1], x3[2]))
                         else:
                             doev(*x3)
+                    nmid = cb == 0 and ci > 1
                     for x3 in accs[0:1]:
-                        evx(x3)
+                        if nmid:
+                            ev_sq(x3[1], x3[2], cur[3])
+                        else:
+                            evx(x3)
                     if cb == 0 and ci > 1:
                         if prev[1] == 2:
-                            ssq(1, prev[3], list(range(H)), 2 * ((ci - 1) % 2))
+                            ssq(1, prev[3], list(range(8, H)), 2 * ((ci - 1) % 2))
                         else:
                             ssq(1, prev[3], list(range(8, 12)), 2 * ((ci - 1) % 2))
                         nrm(ci - 1, prev[0], 1)
                     if cb == 1 and prev[1] == 2:
                         ssq(2, prev[3], list(range(H)), 2 * ((ci - 1) % 2), 1)
                         nrm(ci - 1, prev[0], 2, 1)
+                    if nmid:
+                        for x3 in accs[0:1]:
+                            ev_v(x3[1], x3[2], cur[2], False)
+                    if split:
+                        accs = accs + [domx(ci, hp) for hp in todo[1:]]
+                    xl = [(xu, gg, x_turn(xu, gg)) for (xu, gg) in XL.get((ci, cb), ())]
                     for x3 in accs[1:]:
                         evx(x3)
-                    banks = (((0, 1), (2,), ()), ((0, 1), (2, 3), (4, 5)))[prev[1] - 1][cb]
+                    for (xu, gg, xg) in xlate:
+                        x_quant(xu, gg, xg)
+                    xlate = [(xu, gg, x_copy(xt)) for (xu, gg, xt) in xl]
+                    banks = (((0, 1), (2,), ()), ((0, 1, 2), (3, 4), (5,)))[prev[1] - 1][cb]
                     for bank in banks:
-                        rope(prev[0] + bank // 3, bank // 3, bank % 3, prev[2])
+                        rope(prev[0] + bank // 3, bank // 3, bank % 3, prev[2], ())
+                    if (ci, cb) == (1, 2):
+                        tables(2, TT - 2)
+                    if (ci, cb) == (2, 0):
+                        for xi in x_rest:
+                            x_quant(*xi)
                     for (hp, acc_) in held:
                         ev_v(hp, acc_, cur[2], True)
+                    if cur[1] == 2 and cb == 2:
+                        ssq(1, cur[3], list(range(8)), 2 * (ci % 2))
                     if cur[1] == 1 and cb > 0:
                         ssq(cur[1], cur[3], list(range(4 * cb - 4, 4 * cb)), 2 * (ci % 2))
                         if ci == len(CHUNKS) - 1:

@@ -268,6 +268,12 @@ def tile_causalwanmodel_pa_kernel(tc, x, w_bytes, w_scale, b, g, freqs_cos, freq
                 nc.scalar.activation(out=fin[:], in_=un[:], func=ACT.Copy, scale=rstd[:, i:i + 1])
             nc.sync.dma_start(out=out_rows[i * P:(i + 1) * P, q * NCH:(q + 1) * NCH], in_=fin[:].rearrange("p h j e -> p (h j e)"))
 
+        def keep_warm(wide, n):
+            dummy = ps_t.tile([P, NCH], F32, name="dummy", tag="tp")
+            cols = wide.shape[2]
+            for t in range(n):
+                nc.tensor.matmul(out=dummy[:, 0:cols], lhsT=x_sb[:, 0, 0:P], rhs=wide[:, t, :], start=True, stop=True)
+
         def warm_up(n):
             dummy = ps_t.tile([P, NCH], F32, name="dummy", tag="tp")
             for rep in range(n):
@@ -275,13 +281,14 @@ def tile_causalwanmodel_pa_kernel(tc, x, w_bytes, w_scale, b, g, freqs_cos, freq
 
         V0 = [0,2]
         V1 = []
-        WARM = {3: 4, 6: 4, 9: 4}
+        DW = {4: 3, 5: 3, 8: 3}
+        WARM = {1: 4, 3: 4, 6: 4, 9: 3}
         NV = {}
         VL = {}
         def nrm(ci, t0, nt, first=0):
             (norm_v if (ci, first) in NV else norm)(ci, t0, nt, first)
         XL = {}
-        EX = {}
+        EX = {10: ((1, 0),)}
         with tc.manual_schedule():
             units = [(h0, nh, gg) for (h0, nh) in W_BLOCKS for gg in range(G)]
             xjobs = {0: ((0, 0), (0, 1)), 1: ((0, 2),), 3: ((1, 0),), 4: ((1, 1),), 5: ((1, 2),), 6: ((2, 0),), 8: ((2, 1),), 10: ((2, 2),), 11: ((3, 0), (3, 1), (3, 2))}
@@ -332,17 +339,22 @@ def tile_causalwanmodel_pa_kernel(tc, x, w_bytes, w_scale, b, g, freqs_cos, freq
                         late_x.append(xi)
                 if cur_w is not None:
                     wg = w_mix(cur_w[1], cur_w[3])
+                hold = (7, 8)
                 for (ci, hp, acc) in pend:
-                    doev(ci, hp, acc)
-                    done.add((ci, hp))
-                    if ci == 0:
-                        evd = evd + [2 * hp, 2 * hp + 1]
-                pend = []
+                    if i not in hold:
+                        doev(ci, hp, acc)
+                        done.add((ci, hp))
+                        if ci == 0:
+                            evd = evd + [2 * hp, 2 * hp + 1]
+                if i not in hold:
+                    pend = []
                 if prev_w is not None and prev_w[2] == G - 1:
                     h0, nh = prev_w[0], prev_w[1]
-                    pend = [domx(0, hp) for hp in range(h0 // 2, (h0 + nh) // 2)]
+                    pend = pend + [domx(0, hp) for hp in range(h0 // 2, (h0 + nh) // 2)]
                 for (ci, hp) in EX.get(i, ()):
                     pend.append(domx(ci, hp))
+                if i in DW:
+                    keep_warm(cur_w[3], DW[i])
                 prev_w = (cur_w[0], cur_w[1], cur_w[2], wg) if cur_w is not None else None
                 turned = new_t
                 copied = new_c
@@ -350,7 +362,7 @@ def tile_causalwanmodel_pa_kernel(tc, x, w_bytes, w_scale, b, g, freqs_cos, freq
                 ssq(1, chunk(0)[3], evd, 0)
                 evd = []
             new_c = [(xu, gg, x_copy(xt)) for (xu, gg, xt) in turned]
-            c1 = [domx(1, hp) for hp in (0, 1)]
+            c1 = [domx(1, hp) for hp in (1, 2)]
             for (ci, hp, acc) in pend:
                 doev(ci, hp, acc)
                 done.add((ci, hp))

@@ -11,7 +11,6 @@ FP8 = mybir.dt.float8_e4m3fn
 FP8X4 = mybir.dt.float8_e4m3fn_x4
 ALU = mybir.AluOpType
 ACT = mybir.ActivationFunctionType
-AX = mybir.AxisListType
 
 T = 1024
 D = 1536
@@ -28,6 +27,13 @@ EPS = 1e-6
 FLOPS = 2 * T * D * D
 CHUNKS = ((0, 2), (2, 2), (4, 2), (6, 1), (7, 1))
 W_BLOCKS = ((0, 4), (4, 4), (8, 2), (10, 2))
+X_TURNS = {0: ((0, 0), (0, 1)), 1: ((0, 2),), 3: ((1, 0),), 4: ((1, 1),), 5: ((1, 2),), 6: ((2, 0),), 8: ((2, 1),), 10: ((2, 2),), 11: ((3, 0), (3, 1), (3, 2))}
+WARM_X = {1: 4, 3: 4, 6: 4, 9: 3}
+WARM_W = {4: 3, 5: 3, 8: 3}
+HOLD = (7, 8)
+V_PAIR = 2
+AHEAD_STEP = 10
+RUN = 8
 
 
 def tile_causalwanmodel_pa_kernel(tc, x, w_bytes, w_scale, b, g, freqs_cos, freqs_sin, out):
@@ -68,14 +74,14 @@ def tile_causalwanmodel_pa_kernel(tc, x, w_bytes, w_scale, b, g, freqs_cos, freq
         load_x(0, 1)
         load_x(1, 1)
         load_w(2, slice(0, NCH))
+        load_w(0, slice(NCH, D))
+        load_w(1, slice(NCH, D))
         nc.sync.dma_start(out=bg_rows[0:H, :], in_=b.rearrange("(h p) -> h p", p=P))
         nc.sync.dma_start(out=bg_rows[32:32 + H, :], in_=g.rearrange("(h p) -> h p", p=P))
-        load_w(0, slice(NCH, D))
         load_x(2, 2)
-        load_w(1, slice(NCH, D))
         load_w(2, slice(NCH, D))
-        for i in range(4, TT, 2):
-            load_x(i, 2)
+        load_x(4, 2)
+        load_x(6, 2)
         nc.sync.dma_start(out=cos_sb[:], in_=freqs_cos.rearrange("(i p) j -> p i j", p=P))
         nc.sync.dma_start(out=sin_sb[:], in_=freqs_sin.rearrange("(i p) j -> p i j", p=P))
 
@@ -92,25 +98,24 @@ def tile_causalwanmodel_pa_kernel(tc, x, w_bytes, w_scale, b, g, freqs_cos, freq
         cdup = keep.tile([P, TT * J, 2], F32, name="cdup")
         s3 = keep.tile([P, TT * J, 2], F32, name="s3")
 
-        def tables(i0, n):
-            js = slice(i0 * J, (i0 + n) * J)
-            nc.vector.tensor_copy(out=cdup[:, js, :], in_=cos_sb[:].rearrange("p i j -> p (i j)")[:, js].unsqueeze(2).to_broadcast([P, n * J, 2]))
+        def tables():
+            nc.vector.tensor_copy(out=cdup[:], in_=cos_sb[:].rearrange("p i j -> p (i j)").unsqueeze(2).to_broadcast([P, TT * J, 2]))
             nc.vector.tensor_tensor(
-                out=s3[:, js, :], in0=sin_sb[:].rearrange("p i j -> p (i j)")[:, js].unsqueeze(2).to_broadcast([P, n * J, 2]),
-                in1=sgn[:].unsqueeze(1).to_broadcast([P, n * J, 2]), op=ALU.mult,
+                out=s3[:], in0=sin_sb[:].rearrange("p i j -> p (i j)").unsqueeze(2).to_broadcast([P, TT * J, 2]),
+                in1=sgn[:].unsqueeze(1).to_broadcast([P, TT * J, 2]), op=ALU.mult,
             )
 
         bg_f = keep.tile([P, P], F32, name="bg_f")
         bgc = keep.tile([P, P], F32, name="bgc")
         gb = keep.tile([P, H], F32, name="gb")
 
-        def bias_and_gain():
+        def bias_and_gain_turn():
             nc.vector.tensor_copy(out=bg_f[:], in_=bg_rows[:])
             bg_ps = ps_t.tile([P, P], F32, name="bg_ps", tag="tp")
             nc.tensor.transpose(bg_ps[:], bg_f[:], ident[:])
             return bg_ps
 
-        def bias_and_gain2(bg_ps):
+        def bias_and_gain_copy(bg_ps):
             nc.vector.tensor_copy(out=bgc[:], in_=bg_ps[:])
             nc.vector.tensor_tensor(out=gb[:], in0=bgc[:, 0:H], in1=bgc[:, 32:32 + H], op=ALU.mult)
 
@@ -149,7 +154,7 @@ def tile_causalwanmodel_pa_kernel(tc, x, w_bytes, w_scale, b, g, freqs_cos, freq
 
         def w_mix(nh, wide):
             wg = stage.tile([P, nh * P, PACK], BF16, name="wg", align_bytes=64)
-            nc.vector.tensor_copy(out=wg[:].rearrange("p (c i) t -> p c t i", i=4), in_=wide[:].rearrange("p t (c i) -> p c t i", i=4))
+            nc.vector.tensor_copy(out=wg[:].rearrange("p (c i) t -> p c t i", i=RUN), in_=wide[:].rearrange("p t (c i) -> p c t i", i=RUN))
             return wg
 
         def w_quant(h0, nh, gg, wg):
@@ -160,7 +165,17 @@ def tile_causalwanmodel_pa_kernel(tc, x, w_bytes, w_scale, b, g, freqs_cos, freq
         ms = keep.tile([P, TT], F32, name="ms")
         rstd = keep.tile([P, TT], F32, name="rstd")
 
-        def mx(t0, nt, hp):
+        v_of = {}
+        sq_of = {}
+
+        def open_chunk(ci):
+            v_new = vpool.tile([P, H, CHUNKS[ci][1] * P], F32, name="v")
+            sq_new = sqp.tile([P, H, CHUNKS[ci][1] * P], F32, name="sq")
+            v_of[ci] = v_new
+            sq_of[ci] = sq_new
+
+        def mx(ci, hp):
+            t0, nt = CHUNKS[ci]
             acc = ps_a.tile([P, 2, nt * P], F32, name="acc")
             ts = slice(t0 * P, (t0 + nt) * P)
             for a in range(2):
@@ -174,103 +189,73 @@ def tile_causalwanmodel_pa_kernel(tc, x, w_bytes, w_scale, b, g, freqs_cos, freq
                     )
             return acc
 
-        def ev(hp, acc, v_k, sq_k, v_on_vector):
-            ev_sq(hp, acc, sq_k)
-            ev_v(hp, acc, v_k, v_on_vector)
-
-        def ev_sq(hp, acc, sq_k):
+        def squares(ci, hp, acc):
             for a in range(2):
                 h = 2 * hp + a
-                nc.scalar.activation(out=sq_k[:, h, :], in_=acc[:, a, :], func=ACT.Square, bias=bgc[:, h:h + 1])
+                nc.scalar.activation(out=sq_of[ci][:, h, :], in_=acc[:, a, :], func=ACT.Square, bias=bgc[:, h:h + 1])
 
-        def ev_v(hp, acc, v_k, v_on_vector):
+        def values(ci, hp, acc, on_vector=False):
             for a in range(2):
                 h = 2 * hp + a
-                if v_on_vector:
-                    nc.vector.tensor_scalar(out=v_k[:, h, :], in0=acc[:, a, :], scalar1=bgc[:, 32 + h:33 + h], scalar2=gb[:, h:h + 1], op0=ALU.mult, op1=ALU.add)
+                if on_vector:
+                    nc.vector.tensor_scalar(out=v_of[ci][:, h, :], in0=acc[:, a, :], scalar1=bgc[:, 32 + h:33 + h], scalar2=gb[:, h:h + 1], op0=ALU.mult, op1=ALU.add)
                 else:
-                    nc.scalar.activation(out=v_k[:, h, :], in_=acc[:, a, :], func=ACT.Identity, scale=bgc[:, 32 + h:33 + h], bias=gb[:, h:h + 1])
+                    nc.scalar.activation(out=v_of[ci][:, h, :], in_=acc[:, a, :], func=ACT.Identity, scale=bgc[:, 32 + h:33 + h], bias=gb[:, h:h + 1])
 
-        def ssq(nt, sq_k, heads, base, first=0):
-            for r in range(first, nt):
-                for h in heads:
-                    nc.tensor.matmul(out=ss_ps[:, base + r, :], lhsT=sq_k[:, h, r * P:(r + 1) * P], rhs=ident[:], is_transpose=True, start=(h == 0), stop=(h == H - 1))
+        def square_sum(ci, r, heads):
+            for h in heads:
+                nc.tensor.matmul(out=ss_ps[:, 2 * (ci % 2) + r, :], lhsT=sq_of[ci][:, h, r * P:(r + 1) * P], rhs=ident[:], is_transpose=True, start=(h == 0), stop=(h == H - 1))
 
-        def norm_v(ci, t0, nt, first=0):
-            base = 2 * (ci % 2)
-            isl = slice(t0 + first, t0 + nt)
-            for r in range(first, nt):
-                nc.vector.tensor_reduce(out=ms[:, t0 + r:t0 + r + 1], in_=ss_ps[:, base + r, :], axis=AX.X, op=ALU.add)
-            nc.scalar.activation(out=rstd[:, isl], in_=ms[:, isl], func=ACT.Abs_reciprocal_sqrt, scale=1.0 / D, bias=eps_t[:])
+        def norm(ci, r):
+            i = CHUNKS[ci][0] + r
+            junk = epi.tile([P, P], F32, name="junk")
+            nc.scalar.activation(out=junk[:], in_=ss_ps[:, 2 * (ci % 2) + r, :], func=ACT.Copy, accum_out=ms[:, i:i + 1])
+            nc.scalar.activation(out=rstd[:, i:i + 1], in_=ms[:, i:i + 1], func=ACT.Abs_reciprocal_sqrt, scale=1.0 / D, bias=eps_t[:])
 
-        def norm(ci, t0, nt, first=0):
-            base = 2 * (ci % 2)
-            isl = slice(t0 + first, t0 + nt)
-            for r in range(first, nt):
-                junk = epi.tile([P, P], F32, name="junk")
-                nc.scalar.activation(out=junk[:], in_=ss_ps[:, base + r, :], func=ACT.Copy, accum_out=ms[:, t0 + r:t0 + r + 1])
-            nc.scalar.activation(out=rstd[:, isl], in_=ms[:, isl], func=ACT.Abs_reciprocal_sqrt, scale=1.0 / D, bias=eps_t[:])
+        def bank_back(ci, r, q):
+            bt = ps_t.tile([P, 4, J, 2], F32, name="bt", tag="tp")
+            for hh in range(4):
+                nc.tensor.transpose(bt[:, hh, :, :].rearrange("p j e -> p (j e)"), v_of[ci][:, 4 * q + hh, r * P:(r + 1) * P], ident[:])
+            return bt
+
+        def products(i, bt, scaled):
+            t1 = epi.tile([P, 4, J, 2], F32, name="t1")
+            t2 = epi.tile([P, 4, J, 2], F32, name="t2")
+            cos_in = cdup[:, i * J:(i + 1) * J, :].unsqueeze(1).to_broadcast([P, 4, J, 2])
+            sin_in = s3[:, i * J:(i + 1) * J, :].unsqueeze(1).to_broadcast([P, 4, J, 2])
+            if scaled:
+                nc.vector.scalar_tensor_tensor(out=t1[:], in0=bt[:], scalar=rstd[:, i:i + 1], in1=cos_in, op0=ALU.mult, op1=ALU.mult)
+                nc.vector.scalar_tensor_tensor(out=t2[:], in0=bt[:, :, :, ::-1], scalar=rstd[:, i:i + 1], in1=sin_in, op0=ALU.mult, op1=ALU.mult)
+            else:
+                nc.vector.tensor_tensor(out=t1[:], in0=bt[:], in1=cos_in, op=ALU.mult)
+                nc.vector.tensor_tensor(out=t2[:], in0=bt[:, :, :, ::-1], in1=sin_in, op=ALU.mult)
+            return t1, t2
+
+        def store_bank(i, q, fin):
+            nc.sync.dma_start(out=out_rows[i * P:(i + 1) * P, q * NCH:(q + 1) * NCH], in_=fin[:].rearrange("p h j e -> p (h j e)"))
 
         o_tiles = {}
 
-        def rope(i, r, q, v_k, vadd=()):
-            bt = ps_t.tile([P, 4, J, 2], F32, name="bt", tag="tp")
-            for hh in range(4):
-                nc.tensor.transpose(bt[:, hh, :, :].rearrange("p j e -> p (j e)"), v_k[:, 4 * q + hh, r * P:(r + 1) * P], ident[:])
+        def rope(ci, bank, bt):
+            i = CHUNKS[ci][0] + bank // 3
+            q = bank % 3
             if q == 0:
                 o_new = epi.tile([P, H, J, 2], F32, name="o")
                 o_tiles[i] = o_new
             o = o_tiles[i]
-            t1 = epi.tile([P, 4, J, 2], F32, name="t1")
-            t2 = epi.tile([P, 4, J, 2], F32, name="t2")
-            js = slice(i * J, (i + 1) * J)
-            nc.vector.scalar_tensor_tensor(out=t1[:], in0=bt[:], scalar=rstd[:, i:i + 1], in1=cdup[:, js, :].unsqueeze(1).to_broadcast([P, 4, J, 2]), op0=ALU.mult, op1=ALU.mult)
-            nc.vector.scalar_tensor_tensor(out=t2[:], in0=bt[:, :, :, ::-1], scalar=rstd[:, i:i + 1], in1=s3[:, js, :].unsqueeze(1).to_broadcast([P, 4, J, 2]), op0=ALU.mult, op1=ALU.mult)
-            add_eng = nc.vector if (i, q) in vadd else nc.gpsimd
-            add_eng.tensor_tensor(out=o[:, 4 * q:4 * q + 4, :, :], in0=t1[:], in1=t2[:], op=ALU.add)
-            if i == TT - 1:
-                nc.sync.dma_start(out=out_rows[i * P:(i + 1) * P, q * NCH:(q + 1) * NCH], in_=o[:, 4 * q:4 * q + 4, :, :].rearrange("p h j e -> p (h j e)"))
-            elif q == 2:
+            t1, t2 = products(i, bt, True)
+            nc.gpsimd.tensor_tensor(out=o[:, 4 * q:4 * q + 4, :, :], in0=t1[:], in1=t2[:], op=ALU.add)
+            if q == 2:
                 nc.sync.dma_start(out=out_rows[i * P:(i + 1) * P, :], in_=o[:].rearrange("p h j e -> p (h j e)"))
 
-        def bank_back(r, q, v_k):
-            bt = ps_t.tile([P, 4, J, 2], F32, name="bt", tag="tp")
-            for hh in range(4):
-                nc.tensor.transpose(bt[:, hh, :, :].rearrange("p j e -> p (j e)"), v_k[:, 4 * q + hh, r * P:(r + 1) * P], ident[:])
-            return bt
-
-        def rope_store(i, q, bt, add_engine):
-            t1 = epi.tile([P, 4, J, 2], F32, name="t1")
-            t2 = epi.tile([P, 4, J, 2], F32, name="t2")
+        def last_bank(i, q, bt, add_engine):
+            t1, t2 = products(i, bt, True)
             fin = epi.tile([P, 4, J, 2], F32, name="fin")
-            js = slice(i * J, (i + 1) * J)
-            nc.vector.scalar_tensor_tensor(out=t1[:], in0=bt[:], scalar=rstd[:, i:i + 1], in1=cdup[:, js, :].unsqueeze(1).to_broadcast([P, 4, J, 2]), op0=ALU.mult, op1=ALU.mult)
-            nc.vector.scalar_tensor_tensor(out=t2[:], in0=bt[:, :, :, ::-1], scalar=rstd[:, i:i + 1], in1=s3[:, js, :].unsqueeze(1).to_broadcast([P, 4, J, 2]), op0=ALU.mult, op1=ALU.mult)
             add_engine.tensor_tensor(out=fin[:], in0=t1[:], in1=t2[:], op=ALU.add)
-            nc.sync.dma_start(out=out_rows[i * P:(i + 1) * P, q * NCH:(q + 1) * NCH], in_=fin[:].rearrange("p h j e -> p (h j e)"))
+            store_bank(i, q, fin)
 
-        def rope_unscaled(i, r, q, v_k, add_engine):
-            bt = bank_back(r, q, v_k)
-            t1 = epi.tile([P, 4, J, 2], F32, name="t1")
-            t2 = epi.tile([P, 4, J, 2], F32, name="t2")
-            un = epi.tile([P, 4, J, 2], F32, name="un")
-            js = slice(i * J, (i + 1) * J)
-            nc.vector.tensor_tensor(out=t1[:], in0=bt[:], in1=cdup[:, js, :].unsqueeze(1).to_broadcast([P, 4, J, 2]), op=ALU.mult)
-            nc.vector.tensor_tensor(out=t2[:], in0=bt[:, :, :, ::-1], in1=s3[:, js, :].unsqueeze(1).to_broadcast([P, 4, J, 2]), op=ALU.mult)
-            add_engine.tensor_tensor(out=un[:], in0=t1[:], in1=t2[:], op=ALU.add)
-            return un
-
-        def scale_store(i, q, un, on_vector):
-            fin = epi.tile([P, 4, J, 2], F32, name="fin")
-            if on_vector:
-                nc.vector.tensor_scalar(out=fin[:], in0=un[:], scalar1=rstd[:, i:i + 1], scalar2=None, op0=ALU.mult)
-            else:
-                nc.scalar.activation(out=fin[:], in_=un[:], func=ACT.Copy, scale=rstd[:, i:i + 1])
-            nc.sync.dma_start(out=out_rows[i * P:(i + 1) * P, q * NCH:(q + 1) * NCH], in_=fin[:].rearrange("p h j e -> p (h j e)"))
-
-        def keep_warm(wide, n):
+        def keep_warm(wide, cols, n):
             dummy = ps_t.tile([P, NCH], F32, name="dummy", tag="tp")
-            cols = wide.shape[2]
             for t in range(n):
                 nc.tensor.matmul(out=dummy[:, 0:cols], lhsT=x_sb[:, 0, 0:P], rhs=wide[:, t, :], start=True, stop=True)
 
@@ -279,176 +264,118 @@ def tile_causalwanmodel_pa_kernel(tc, x, w_bytes, w_scale, b, g, freqs_cos, freq
             for rep in range(n):
                 nc.tensor.matmul(out=dummy[:], lhsT=x_sb[:, 0, 0:P], rhs=x_sb[:, 0, 0:NCH], start=True, stop=True)
 
-        V0 = [0,2]
-        V1 = []
-        DW = {4: 3, 5: 3, 8: 3}
-        WARM = {1: 4, 3: 4, 6: 4, 9: 3}
-        NV = {}
-        VL = {}
-        def nrm(ci, t0, nt, first=0):
-            (norm_v if (ci, first) in NV else norm)(ci, t0, nt, first)
-        XL = {}
-        EX = {10: ((1, 0),)}
         with tc.manual_schedule():
+            for ci in range(2):
+                open_chunk(ci)
             units = [(h0, nh, gg) for (h0, nh) in W_BLOCKS for gg in range(G)]
-            xjobs = {0: ((0, 0), (0, 1)), 1: ((0, 2),), 3: ((1, 0),), 4: ((1, 1),), 5: ((1, 2),), 6: ((2, 0),), 8: ((2, 1),), 10: ((2, 2),), 11: ((3, 0), (3, 1), (3, 2))}
-            vs = {}
-            def chunk(ci):
-                if ci not in vs:
-                    nt_ = CHUNKS[ci][1]
-                    v_new = vpool.tile([P, H, nt_ * P], F32, name="v")
-                    sq_new = sqp.tile([P, H, nt_ * P], F32, name="sq")
-                    vs[ci] = (CHUNKS[ci][0], nt_, v_new, sq_new)
-                return vs[ci]
-            def domx(ci, hp):
-                t0_, nt_, v_, sq_ = chunk(ci)
-                return (ci, hp, mx(t0_, nt_, hp))
-            def doev(ci, hp, acc):
-                t0_, nt_, v_, sq_ = chunk(ci)
-                ev(hp, acc, v_, sq_, (ci == 0 and hp in V0) or (ci == 1 and hp in V1))
             done = set()
-            prev_w = None
+            mixed = None
             turned = []
             copied = []
             late_x = []
             pend = []
-            evd = []
-            n1 = len(units)
-            for i in range(n1 + 1):
-                cur_w = None
-                if i < n1:
-                    h0, nh, gg = units[i]
-                    cur_w = (h0, nh, gg, w_widen(h0, nh, gg, {0: 3, 2: 2, 5: 2, 8: 2, 11: 2}.get(i, 1)))
-                new_t = [(xu, gg, x_turn(xu, gg)) for (xu, gg) in xjobs.get(i, ())]
+            sums = []
+            for step in range(len(units) + 1):
+                if step < len(units):
+                    h0, nh, gg = units[step]
+                    wide = w_widen(h0, nh, gg, 3 if step == 0 else 2 if gg == G - 1 else 1)
+                new_t = [(xu, gg, x_turn(xu, gg)) for (xu, gg) in X_TURNS.get(step, ())]
                 new_c = [(xu, gg, x_copy(xt)) for (xu, gg, xt) in turned]
-                if i == 2:
-                    bg_ps = bias_and_gain()
-                if i == 3:
-                    bias_and_gain2(bg_ps)
-                if evd:
-                    ssq(1, chunk(0)[3], evd, 0)
-                    evd = []
-                if i in WARM:
-                    warm_up(WARM[i])
-                if prev_w is not None:
-                    w_quant(prev_w[0], prev_w[1], prev_w[2], prev_w[3])
-                for xi in copied:
-                    if xi[0] < 2:
-                        x_quant(*xi)
+                if step == 2:
+                    bg_ps = bias_and_gain_turn()
+                if step == 3:
+                    bias_and_gain_copy(bg_ps)
+                square_sum(0, 0, sums)
+                sums = []
+                if step in WARM_X:
+                    warm_up(WARM_X[step])
+                if mixed is not None:
+                    w_quant(*mixed)
+                for job in copied:
+                    if job[0] < 2:
+                        x_quant(*job)
                     else:
-                        late_x.append(xi)
-                if cur_w is not None:
-                    wg = w_mix(cur_w[1], cur_w[3])
-                hold = (7, 8)
-                for (ci, hp, acc) in pend:
-                    if i not in hold:
-                        doev(ci, hp, acc)
+                        late_x.append(job)
+                if step < len(units):
+                    h0, nh, gg = units[step]
+                    wg = w_mix(nh, wide)
+                if step not in HOLD:
+                    for (ci, hp, acc) in pend:
+                        squares(ci, hp, acc)
+                        values(ci, hp, acc, ci == 0 and hp == V_PAIR)
                         done.add((ci, hp))
                         if ci == 0:
-                            evd = evd + [2 * hp, 2 * hp + 1]
-                if i not in hold:
+                            sums = sums + [2 * hp, 2 * hp + 1]
                     pend = []
-                if prev_w is not None and prev_w[2] == G - 1:
-                    h0, nh = prev_w[0], prev_w[1]
-                    pend = pend + [domx(0, hp) for hp in range(h0 // 2, (h0 + nh) // 2)]
-                for (ci, hp) in EX.get(i, ()):
-                    pend.append(domx(ci, hp))
-                if i in DW:
-                    keep_warm(cur_w[3], DW[i])
-                prev_w = (cur_w[0], cur_w[1], cur_w[2], wg) if cur_w is not None else None
+                if mixed is not None and mixed[2] == G - 1:
+                    pend = pend + [(0, hp, mx(0, hp)) for hp in range(mixed[0] // 2, (mixed[0] + mixed[1]) // 2)]
+                if step == AHEAD_STEP:
+                    pend.append((1, 0, mx(1, 0)))
+                if step in WARM_W:
+                    keep_warm(wide, units[step][1] * P, WARM_W[step])
+                mixed = (h0, nh, gg, wg) if step < len(units) else None
                 turned = new_t
                 copied = new_c
-            if evd:
-                ssq(1, chunk(0)[3], evd, 0)
-                evd = []
-            new_c = [(xu, gg, x_copy(xt)) for (xu, gg, xt) in turned]
-            c1 = [domx(1, hp) for hp in (1, 2)]
+
+            square_sum(0, 0, sums)
+            sums = []
+            copied = copied + [(xu, gg, x_copy(xt)) for (xu, gg, xt) in turned]
+            ahead = [(1, hp, mx(1, hp)) for hp in (1, 2)]
+            early = {q: bank_back(0, 0, q) for q in range(2)}
             for (ci, hp, acc) in pend:
-                doev(ci, hp, acc)
+                squares(ci, hp, acc)
+                values(ci, hp, acc)
                 done.add((ci, hp))
                 if ci == 0:
-                    evd = evd + [2 * hp, 2 * hp + 1]
-            for x3 in c1[0:1]:
-                ev_sq(x3[1], x3[2], chunk(1)[3])
-            ssq(1, chunk(0)[3], evd, 0)
-            nrm(0, 0, 1)
-            for x3 in c1[0:1]:
-                ev_v(x3[1], x3[2], chunk(1)[2], False)
-            for x3 in c1[1:]:
-                doev(*x3)
-            for x3 in c1:
-                done.add((x3[0], x3[1]))
-            x_rest = late_x + copied + new_c
-            for xi in [xi for xi in x_rest if xi[0] < 4]:
-                x_quant(*xi)
-            x_rest = [xi for xi in x_rest if xi[0] >= 4]
-            tables(0, 2)
-            for xi in x_rest[0:0]:
-                x_quant(*xi)
-            x_rest = x_rest[0:]
-            prev = chunk(0)
-            late = []
-            xlate = []
-            for ci in range(1, len(CHUNKS)):
-                cur = chunk(ci)
+                    sums = sums + [2 * hp, 2 * hp + 1]
+            squares(*ahead[0])
+            square_sum(0, 0, sums)
+            norm(0, 0)
+            values(*ahead[0])
+            squares(*ahead[1])
+            values(*ahead[1])
+            for (ci, hp, acc) in ahead:
+                done.add((ci, hp))
+            for job in late_x + copied:
+                x_quant(*job)
+            tables()
+
+            last = len(CHUNKS) - 1
+            late = {}
+            for ci in range(1, last + 1):
+                if ci > 1:
+                    open_chunk(ci)
+                pc = ci - 1
+                pair = CHUNKS[pc][1] == 2
                 for cb in range(3):
-                    held = []
-                    todo = [hp for hp in (2 * cb, 2 * cb + 1) if (ci, hp) not in done]
-                    split = cb == 0 and ci == 2
-                    accs = [domx(ci, hp) for hp in (todo[0:1] if split else todo)]
-                    def evx(x3):
-                        if (x3[0], x3[1]) in VL:
-                            ev_sq(x3[1], x3[2], cur[3])
-                            held.append((x3[1], x3[2]))
-                        else:
-                            doev(*x3)
-                    nmid = cb == 0 and ci > 1
-                    for x3 in accs[0:1]:
-                        if nmid:
-                            ev_sq(x3[1], x3[2], cur[3])
-                        else:
-                            evx(x3)
-                    if cb == 0 and ci > 1:
-                        if prev[1] == 2:
-                            ssq(1, prev[3], list(range(8, H)), 2 * ((ci - 1) % 2))
-                        else:
-                            ssq(1, prev[3], list(range(8, 12)), 2 * ((ci - 1) % 2))
-                        nrm(ci - 1, prev[0], 1)
-                    if cb == 1 and prev[1] == 2:
-                        ssq(2, prev[3], list(range(H)), 2 * ((ci - 1) % 2), 1)
-                        nrm(ci - 1, prev[0], 2, 1)
-                    if nmid:
-                        for x3 in accs[0:1]:
-                            ev_v(x3[1], x3[2], cur[2], False)
-                    if split:
-                        accs = accs + [domx(ci, hp) for hp in todo[1:]]
-                    xl = [(xu, gg, x_turn(xu, gg)) for (xu, gg) in XL.get((ci, cb), ())]
-                    for x3 in accs[1:]:
-                        evx(x3)
-                    for (xu, gg, xg) in xlate:
-                        x_quant(xu, gg, xg)
-                    xlate = [(xu, gg, x_copy(xt)) for (xu, gg, xt) in xl]
-                    banks = (((0, 1), (2,), ()), ((0, 1, 2), (3, 4), (5,)))[prev[1] - 1][cb]
-                    for bank in banks:
-                        rope(prev[0] + bank // 3, bank // 3, bank % 3, prev[2], ())
-                    if (ci, cb) == (1, 2):
-                        tables(2, TT - 2)
-                    if (ci, cb) == (2, 0):
-                        for xi in x_rest:
-                            x_quant(*xi)
-                    for (hp, acc_) in held:
-                        ev_v(hp, acc_, cur[2], True)
-                    if cur[1] == 2 and cb == 2:
-                        ssq(1, cur[3], list(range(8)), 2 * (ci % 2))
-                    if cur[1] == 1 and cb > 0:
-                        ssq(cur[1], cur[3], list(range(4 * cb - 4, 4 * cb)), 2 * (ci % 2))
-                        if ci == len(CHUNKS) - 1:
-                            late.append(rope_unscaled(cur[0], 0, 0, cur[2], nc.gpsimd) if cb == 1 else bank_back(0, 1, cur[2]))
-                prev = cur
-            ci = len(CHUNKS)
-            late.append(bank_back(0, 2, prev[2]))
-            ssq(prev[1], prev[3], list(range(8, 12)), 2 * ((ci - 1) % 2))
-            norm(ci - 1, prev[0], prev[1])
-            scale_store(prev[0], 0, late[0], False)
-            rope_store(prev[0], 1, late[1], nc.gpsimd)
-            rope_store(prev[0], 2, late[2], nc.vector)
+                    accs = [(ci, hp, mx(ci, hp)) for hp in (2 * cb, 2 * cb + 1) if (ci, hp) not in done]
+                    for a in accs[0:1]:
+                        squares(*a)
+                        values(*a)
+                    if cb == 0 and pc > 0:
+                        square_sum(pc, 0, range(H) if pair else range(8, H))
+                        norm(pc, 0)
+                    if cb == 1 and pair:
+                        square_sum(pc, 1, range(H))
+                        norm(pc, 1)
+                    for a in accs[1:]:
+                        squares(*a)
+                        values(*a)
+                    for bank in (((0, 1, 2), (3, 4), (5,)) if pair else ((0, 1), (2,), ()))[cb]:
+                        rope(pc, bank, early[bank] if (pc == 0 and bank in early) else bank_back(pc, bank // 3, bank % 3))
+                    if CHUNKS[ci][1] == 1 and cb > 0:
+                        square_sum(ci, 0, range(4 * cb - 4, 4 * cb))
+                    if ci == last and cb == 1:
+                        t1, t2 = products(TT - 1, bank_back(last, 0, 0), False)
+                        un = epi.tile([P, 4, J, 2], F32, name="un")
+                        nc.vector.tensor_tensor(out=un[:], in0=t1[:], in1=t2[:], op=ALU.add)
+                    if ci == last and cb == 2:
+                        late[1] = bank_back(last, 0, 1)
+            late[2] = bank_back(last, 0, 2)
+            square_sum(last, 0, range(8, H))
+            norm(last, 0)
+            fin = epi.tile([P, 4, J, 2], F32, name="fin")
+            nc.scalar.activation(out=fin[:], in_=un[:], func=ACT.Copy, scale=rstd[:, TT - 1:TT])
+            store_bank(TT - 1, 0, fin)
+            last_bank(TT - 1, 1, late[1], nc.gpsimd)
+            last_bank(TT - 1, 2, late[2], nc.vector)

@@ -33,7 +33,7 @@ WARM_W = {4: 3, 5: 3, 8: 3}
 HOLD = (7, 8)
 V_PAIR = 2
 AHEAD_STEP = 10
-RUN = 8
+RUN = 2
 
 
 def tile_causalwanmodel_pa_kernel(tc, x, w_bytes, w_scale, b, g, freqs_cos, freqs_sin, out):

@@ -27,13 +27,13 @@ EPS = 1e-6
 FLOPS = 2 * T * D * D
 CHUNKS = ((0, 2), (2, 2), (4, 2), (6, 1), (7, 1))
 W_BLOCKS = ((0, 4), (4, 4), (8, 2), (10, 2))
-X_TURNS = {0: ((0, 0), (0, 1)), 1: ((0, 2),), 3: ((1, 0),), 4: ((1, 1),), 5: ((1, 2),), 6: ((2, 0),), 8: ((2, 1),), 10: ((2, 2),), 11: ((3, 0), (3, 1), (3, 2))}
+X_TURNS = {0: ((0, 0), (0, 1)), 1: ((0, 2),), 4: ((1, 0),), 5: ((1, 1),), 6: ((1, 2),), 8: ((2, 0),), 9: ((2, 1),), 10: ((2, 2),), 11: ((3, 0), (3, 1), (3, 2))}
 WARM_X = {1: 4, 3: 4, 6: 4, 9: 3}
 WARM_W = {4: 3, 5: 3, 8: 3}
 HOLD = (7, 8)
-V_PAIR = 2
+V_PAIRS = (0, 2)
 AHEAD_STEP = 10
-RUN = 2
+RUN = 4
 
 
 def tile_causalwanmodel_pa_kernel(tc, x, w_bytes, w_scale, b, g, freqs_cos, freqs_sin, out):
@@ -74,10 +74,10 @@ def tile_causalwanmodel_pa_kernel(tc, x, w_bytes, w_scale, b, g, freqs_cos, freq
         load_x(0, 1)
         load_x(1, 1)
         load_w(2, slice(0, NCH))
-        load_w(0, slice(NCH, D))
-        load_w(1, slice(NCH, D))
         nc.sync.dma_start(out=bg_rows[0:H, :], in_=b.rearrange("(h p) -> h p", p=P))
         nc.sync.dma_start(out=bg_rows[32:32 + H, :], in_=g.rearrange("(h p) -> h p", p=P))
+        load_w(0, slice(NCH, D))
+        load_w(1, slice(NCH, D))
         load_x(2, 2)
         load_w(2, slice(NCH, D))
         load_x(4, 2)
@@ -119,10 +119,10 @@ def tile_causalwanmodel_pa_kernel(tc, x, w_bytes, w_scale, b, g, freqs_cos, freq
             nc.vector.tensor_copy(out=bgc[:], in_=bg_ps[:])
             nc.vector.tensor_tensor(out=gb[:], in0=bgc[:, 0:H], in1=bgc[:, 32:32 + H], op=ALU.mult)
 
-        w_codes = keep.tile([P, G, D], U32, name="w_codes", align_bytes=64)
-        w_scl = keep.tile([P, G, D], U8, name="w_scl", align_bytes=64)
-        x_codes = keep.tile([P, G, T], U32, name="x_codes", align_bytes=64)
-        x_scl = keep.tile([P, G, T], U8, name="x_scl", align_bytes=64)
+        w_codes = keep.tile([P, G, D], U32, name="w_codes", align_bytes=256)
+        w_scl = keep.tile([P, G, D], U8, name="w_scl", align_bytes=256)
+        x_codes = keep.tile([P, G, T], U32, name="x_codes", align_bytes=256)
+        x_scl = keep.tile([P, G, T], U8, name="x_scl", align_bytes=256)
 
         def x_turn(xu, gg):
             xt = ps_t.tile([P, 2, XU], F32, name="xt", tag="tp")
@@ -302,7 +302,7 @@ def tile_causalwanmodel_pa_kernel(tc, x, w_bytes, w_scale, b, g, freqs_cos, freq
                 if step not in HOLD:
                     for (ci, hp, acc) in pend:
                         squares(ci, hp, acc)
-                        values(ci, hp, acc, ci == 0 and hp == V_PAIR)
+                        values(ci, hp, acc, ci == 0 and hp in V_PAIRS)
                         done.add((ci, hp))
                         if ci == 0:
                             sums = sums + [2 * hp, 2 * hp + 1]

@@ -119,10 +119,10 @@ def tile_causalwanmodel_pa_kernel(tc, x, w_bytes, w_scale, b, g, freqs_cos, freq
             nc.vector.tensor_copy(out=bgc[:], in_=bg_ps[:])
             nc.vector.tensor_tensor(out=gb[:], in0=bgc[:, 0:H], in1=bgc[:, 32:32 + H], op=ALU.mult)
 
-        w_codes = keep.tile([P, G, D], U32, name="w_codes", align_bytes=256)
-        w_scl = keep.tile([P, G, D], U8, name="w_scl", align_bytes=256)
-        x_codes = keep.tile([P, G, T], U32, name="x_codes", align_bytes=256)
-        x_scl = keep.tile([P, G, T], U8, name="x_scl", align_bytes=256)
+        w_codes = keep.tile([P, G, D], U32, name="w_codes", align_bytes=64)
+        w_scl = keep.tile([P, G, D], U8, name="w_scl", align_bytes=64)
+        x_codes = keep.tile([P, G, T], U32, name="x_codes", align_bytes=64)
+        x_scl = keep.tile([P, G, T], U8, name="x_scl", align_bytes=64)
 
         def x_turn(xu, gg):
             xt = ps_t.tile([P, 2, XU], F32, name="xt", tag="tp")
@@ -202,9 +202,13 @@ def tile_causalwanmodel_pa_kernel(tc, x, w_bytes, w_scale, b, g, freqs_cos, freq
                 else:
                     nc.scalar.activation(out=v_of[ci][:, h, :], in_=acc[:, a, :], func=ACT.Identity, scale=bgc[:, 32 + h:33 + h], bias=gb[:, h:h + 1])
 
-        def square_sum(ci, r, heads):
+        def fold(ci, r, h0, h1, n):
+            sq = sq_of[ci][:, :, r * P:(r + 1) * P]
+            nc.vector.tensor_tensor(out=sq[:, h0:h0 + n, :], in0=sq[:, h0:h0 + n, :], in1=sq[:, h1:h1 + n, :], op=ALU.add)
+
+        def square_sum(ci, r, heads, last_head=H - 1):
             for h in heads:
-                nc.tensor.matmul(out=ss_ps[:, 2 * (ci % 2) + r, :], lhsT=sq_of[ci][:, h, r * P:(r + 1) * P], rhs=ident[:], is_transpose=True, start=(h == 0), stop=(h == H - 1))
+                nc.tensor.matmul(out=ss_ps[:, 2 * (ci % 2) + r, :], lhsT=sq_of[ci][:, h, r * P:(r + 1) * P], rhs=ident[:], is_transpose=True, start=(h == 0), stop=(h == last_head))
 
         def norm(ci, r):
             i = CHUNKS[ci][0] + r
@@ -353,22 +357,30 @@ def tile_causalwanmodel_pa_kernel(tc, x, w_bytes, w_scale, b, g, freqs_cos, freq
                         squares(*a)
                         values(*a)
                     if cb == 0 and pc > 0:
-                        square_sum(pc, 0, range(H) if pair else range(8, H))
+                        square_sum(pc, 0, range(8, H))
                         norm(pc, 0)
                     if cb == 1 and pair:
-                        square_sum(pc, 1, range(H))
+                        if pc > 0:
+                            square_sum(pc, 1, range(3), 2)
+                        else:
+                            square_sum(pc, 1, range(H))
                         norm(pc, 1)
                     for a in accs[1:]:
                         squares(*a)
                         values(*a)
+                    if cb == 0 and pair and (pc > 0):
+                        fold(pc, 1, 0, 6, 6)
+                        fold(pc, 1, 0, 3, 3)
                     for bank in (((0, 1, 2), (3, 4), (5,)) if pair else ((0, 1), (2,), ()))[cb]:
                         rope(pc, bank, early[bank] if (pc == 0 and bank in early) else bank_back(pc, bank // 3, bank % 3))
+                    if CHUNKS[ci][1] == 2 and cb == 2:
+                        square_sum(ci, 0, range(8))
                     if CHUNKS[ci][1] == 1 and cb > 0:
                         square_sum(ci, 0, range(4 * cb - 4, 4 * cb))
                     if ci == last and cb == 1:
                         t1, t2 = products(TT - 1, bank_back(last, 0, 0), False)
                         un = epi.tile([P, 4, J, 2], F32, name="un")
-                        nc.vector.tensor_tensor(out=un[:], in0=t1[:], in1=t2[:], op=ALU.add)
+                        nc.gpsimd.tensor_tensor(out=un[:], in0=t1[:], in1=t2[:], op=ALU.add)
                     if ci == last and cb == 2:
                         late[1] = bank_back(last, 0, 1)
             late[2] = bank_back(last, 0, 2)

@@ -27,7 +27,7 @@ EPS = 1e-6
 FLOPS = 2 * T * D * D
 CHUNKS = ((0, 2), (2, 2), (4, 2), (6, 1), (7, 1))
 W_BLOCKS = ((0, 4), (4, 4), (8, 2), (10, 2))
-X_TURNS = {0: ((0, 0), (0, 1)), 1: ((0, 2),), 4: ((1, 0),), 5: ((1, 1),), 6: ((1, 2),), 8: ((2, 0),), 9: ((2, 1),), 10: ((2, 2),), 11: ((3, 0), (3, 1), (3, 2))}
+X_TURNS = {0: ((0, 0), (0, 1)), 1: ((0, 2),), 3: ((1, 0),), 4: ((1, 1),), 5: ((1, 2),), 6: ((2, 0),), 8: ((2, 1),), 10: ((2, 2),), 11: ((3, 0), (3, 1), (3, 2))}
 WARM_X = {1: 4, 3: 4, 6: 4, 9: 3}
 WARM_W = {4: 3, 5: 3, 8: 3}
 HOLD = (7, 8)
@@ -77,8 +77,8 @@ def tile_causalwanmodel_pa_kernel(tc, x, w_bytes, w_scale, b, g, freqs_cos, freq
         nc.sync.dma_start(out=bg_rows[0:H, :], in_=b.rearrange("(h p) -> h p", p=P))
         nc.sync.dma_start(out=bg_rows[32:32 + H, :], in_=g.rearrange("(h p) -> h p", p=P))
         load_w(0, slice(NCH, D))
-        load_w(1, slice(NCH, D))
         load_x(2, 2)
+        load_w(1, slice(NCH, D))
         load_w(2, slice(NCH, D))
         load_x(4, 2)
         load_x(6, 2)
@@ -202,13 +202,9 @@ def tile_causalwanmodel_pa_kernel(tc, x, w_bytes, w_scale, b, g, freqs_cos, freq
                 else:
                     nc.scalar.activation(out=v_of[ci][:, h, :], in_=acc[:, a, :], func=ACT.Identity, scale=bgc[:, 32 + h:33 + h], bias=gb[:, h:h + 1])
 
-        def fold(ci, r, h0, h1, n):
-            sq = sq_of[ci][:, :, r * P:(r + 1) * P]
-            nc.vector.tensor_tensor(out=sq[:, h0:h0 + n, :], in0=sq[:, h0:h0 + n, :], in1=sq[:, h1:h1 + n, :], op=ALU.add)
-
-        def square_sum(ci, r, heads, last_head=H - 1):
+        def square_sum(ci, r, heads):
             for h in heads:
-                nc.tensor.matmul(out=ss_ps[:, 2 * (ci % 2) + r, :], lhsT=sq_of[ci][:, h, r * P:(r + 1) * P], rhs=ident[:], is_transpose=True, start=(h == 0), stop=(h == last_head))
+                nc.tensor.matmul(out=ss_ps[:, 2 * (ci % 2) + r, :], lhsT=sq_of[ci][:, h, r * P:(r + 1) * P], rhs=ident[:], is_transpose=True, start=(h == 0), stop=(h == H - 1))
 
         def norm(ci, r):
             i = CHUNKS[ci][0] + r
@@ -360,17 +356,11 @@ def tile_causalwanmodel_pa_kernel(tc, x, w_bytes, w_scale, b, g, freqs_cos, freq
                         square_sum(pc, 0, range(8, H))
                         norm(pc, 0)
                     if cb == 1 and pair:
-                        if pc > 0:
-                            square_sum(pc, 1, range(3), 2)
-                        else:
-                            square_sum(pc, 1, range(H))
+                        square_sum(pc, 1, range(H))
                         norm(pc, 1)
                     for a in accs[1:]:
                         squares(*a)
                         values(*a)
-                    if cb == 0 and pair and (pc > 0):
-                        fold(pc, 1, 0, 6, 6)
-                        fold(pc, 1, 0, 3, 3)
                     for bank in (((0, 1, 2), (3, 4), (5,)) if pair else ((0, 1), (2,), ()))[cb]:
                         rope(pc, bank, early[bank] if (pc == 0 and bank in early) else bank_back(pc, bank // 3, bank % 3))
                     if CHUNKS[ci][1] == 2 and cb == 2:

from contextlib import ExitStack

import concourse.mybir as mybir
from concourse.masks import make_identity

F32 = mybir.dt.float32
BF16 = mybir.dt.bfloat16
U32 = mybir.dt.uint32
U8 = mybir.dt.uint8
FP8 = mybir.dt.float8_e4m3fn
FP8X4 = mybir.dt.float8_e4m3fn_x4
ALU = mybir.AluOpType
ACT = mybir.ActivationFunctionType

T = 1024
D = 1536
H = 12
J = 64
P = 128
PACK = 4
K_PASS = P * PACK
G = D // K_PASS
NCH = 512
TT = T // P
XU = 256
EPS = 1e-6
FLOPS = 2 * T * D * D
CHUNKS = ((0, 2), (2, 2), (4, 2), (6, 1), (7, 1))
W_BLOCKS = ((0, 4), (4, 4), (8, 2), (10, 2))
X_TURNS = {0: ((0, 0), (0, 1)), 1: ((0, 2),), 3: ((1, 0),), 4: ((1, 1),), 5: ((1, 2),), 6: ((2, 0),), 8: ((2, 1),), 10: ((2, 2),), 11: ((3, 0), (3, 1), (3, 2))}
WARM_X = {1: 4, 3: 4, 6: 4, 9: 3}
WARM_W = {4: 3, 5: 3, 8: 3}
HOLD = (7, 8)
V_PAIRS = (0, 2)
AHEAD_STEP = 10
RUN = 4


def tile_causalwanmodel_pa_kernel(tc, x, w_bytes, w_scale, b, g, freqs_cos, freqs_sin, out):
    nc = tc.nc
    x_rows = x.rearrange("o t k -> (o t) k")
    out_rows = out.rearrange("o t h d -> (o t) (h d)")
    w_view = w_bytes.rearrange("(g p t) n -> g p t n", p=P, t=PACK)

    with ExitStack() as ctx:
        keep = ctx.enter_context(tc.tile_pool(name="keep", bufs=1))
        stage = ctx.enter_context(tc.tile_pool(name="stage", bufs=3))
        xst = ctx.enter_context(tc.tile_pool(name="xst", bufs=6))
        vpool = ctx.enter_context(tc.tile_pool(name="vpool", bufs=3))
        sqp = ctx.enter_context(tc.tile_pool(name="sqp", bufs=2))
        epi = ctx.enter_context(tc.tile_pool(name="epi", bufs=3))
        ps_t = ctx.enter_context(tc.psum_pool(name="ps_t", bufs=4))
        ps_a = ctx.enter_context(tc.psum_pool(name="ps_a", bufs=3))
        ps_s = ctx.enter_context(tc.psum_pool(name="ps_s", bufs=1))

        cos_sb = keep.tile([P, TT, J], BF16, name="cos_sb")
        sin_sb = keep.tile([P, TT, J], BF16, name="sin_sb")
        bg_rows = keep.tile([P, P], BF16, name="bg_rows")
        nc.vector.memset(bg_rows[:], 0.0)

        wsc = keep.tile([P, G, PACK], F32, name="wsc")
        nc.scalar.dma_start(out=wsc[:], in_=w_scale.rearrange("(g p t) o -> p g (t o)", p=P, t=PACK))
        wb = keep.tile([P, G, PACK, D], U8, name="w_bytes_sb")
        x_sb = keep.tile([P, TT, D], BF16, name="x_sb")

        def load_w(gg, cols):
            nc.sync.dma_start(out=wb[:, gg, :, cols], in_=w_view[gg][:, :, cols])

        def load_x(i, n):
            nc.sync.dma_start(out=x_sb[:, i:i + n, :], in_=x_rows[i * P:(i + n) * P, :].rearrange("(i p) k -> p i k", p=P))

        load_w(0, slice(0, NCH))
        load_w(1, slice(0, NCH))
        load_x(0, 1)
        load_x(1, 1)
        load_w(2, slice(0, NCH))
        nc.sync.dma_start(out=bg_rows[0:H, :], in_=b.rearrange("(h p) -> h p", p=P))
        nc.sync.dma_start(out=bg_rows[32:32 + H, :], in_=g.rearrange("(h p) -> h p", p=P))
        load_w(0, slice(NCH, D))
        load_x(2, 2)
        load_w(1, slice(NCH, D))
        load_w(2, slice(NCH, D))
        load_x(4, 2)
        load_x(6, 2)
        nc.sync.dma_start(out=cos_sb[:], in_=freqs_cos.rearrange("(i p) j -> p i j", p=P))
        nc.sync.dma_start(out=sin_sb[:], in_=freqs_sin.rearrange("(i p) j -> p i j", p=P))

        sgn = keep.tile([P, 2], F32, name="sgn")
        nc.vector.memset(sgn[:, 0:1], -1.0)
        nc.vector.memset(sgn[:, 1:2], 1.0)
        eps_t = keep.tile([P, 1], F32, name="eps_t")
        nc.vector.memset(eps_t[:], EPS)
        warm = keep.tile([P, 1], F32, name="warm")
        nc.scalar.activation(out=warm[:], in_=sgn[:, 1:2], func=ACT.Abs_reciprocal_sqrt)
        ident = keep.tile([P, P], F32, name="ident")
        make_identity(nc, ident[:])

        cdup = keep.tile([P, TT * J, 2], F32, name="cdup")
        s3 = keep.tile([P, TT * J, 2], F32, name="s3")

        def tables():
            nc.vector.tensor_copy(out=cdup[:], in_=cos_sb[:].rearrange("p i j -> p (i j)").unsqueeze(2).to_broadcast([P, TT * J, 2]))
            nc.vector.tensor_tensor(
                out=s3[:], in0=sin_sb[:].rearrange("p i j -> p (i j)").unsqueeze(2).to_broadcast([P, TT * J, 2]),
                in1=sgn[:].unsqueeze(1).to_broadcast([P, TT * J, 2]), op=ALU.mult,
            )

        bg_f = keep.tile([P, P], F32, name="bg_f")
        bgc = keep.tile([P, P], F32, name="bgc")
        gb = keep.tile([P, H], F32, name="gb")

        def bias_and_gain_turn():
            nc.vector.tensor_copy(out=bg_f[:], in_=bg_rows[:])
            bg_ps = ps_t.tile([P, P], F32, name="bg_ps", tag="tp")
            nc.tensor.transpose(bg_ps[:], bg_f[:], ident[:])
            return bg_ps

        def bias_and_gain_copy(bg_ps):
            nc.vector.tensor_copy(out=bgc[:], in_=bg_ps[:])
            nc.vector.tensor_tensor(out=gb[:], in0=bgc[:, 0:H], in1=bgc[:, 32:32 + H], op=ALU.mult)

        w_codes = keep.tile([P, G, D], U32, name="w_codes", align_bytes=64)
        w_scl = keep.tile([P, G, D], U8, name="w_scl", align_bytes=64)
        x_codes = keep.tile([P, G, T], U32, name="x_codes", align_bytes=64)
        x_scl = keep.tile([P, G, T], U8, name="x_scl", align_bytes=64)

        def x_turn(xu, gg):
            xt = ps_t.tile([P, 2, XU], F32, name="xt", tag="tp")
            for r in range(2):
                words = x_sb[:, 2 * xu + r, :].bitcast(F32)
                for u in range(2):
                    nc.tensor.transpose(xt[:, u, r * P:(r + 1) * P], words[:, 256 * gg + u:256 * (gg + 1):2], ident[:])
            return xt

        def x_copy(xt):
            xg = xst.tile([P, XU * PACK], BF16, name="xg", align_bytes=64)
            nc.scalar.copy(out=xg[:].bitcast(F32).rearrange("p (r u) -> p r u", u=2), in_=xt[:].rearrange("p u r -> p r u"))
            return xg

        def x_quant(xu, gg, xg):
            xs = slice(xu * XU, (xu + 1) * XU)
            nc.vector.quantize_mx(out=x_codes[:, gg, xs].bitcast(FP8X4), scales=x_scl[:, gg, xs], in_=xg[:])

        def w_widen(h0, nh, gg, on_vector=1):
            cs = slice(h0 * P, (h0 + nh) * P)
            wide = stage.tile([P, PACK, nh * P], BF16, name="wide")
            for t in range(PACK):
                src = wb[:, gg, t, cs].bitcast(FP8)
                if t >= PACK - on_vector:
                    nc.vector.tensor_scalar(out=wide[:, t, :], in0=src, scalar1=wsc[:, gg, t:t + 1], scalar2=None, op0=ALU.mult)
                else:
                    nc.scalar.activation(out=wide[:, t, :], in_=src, func=ACT.Copy, scale=wsc[:, gg, t:t + 1])
            return wide

        def w_mix(nh, wide):
            wg = stage.tile([P, nh * P, PACK], BF16, name="wg", align_bytes=64)
            nc.vector.tensor_copy(out=wg[:].rearrange("p (c i) t -> p c t i", i=RUN), in_=wide[:].rearrange("p t (c i) -> p c t i", i=RUN))
            return wg

        def w_quant(h0, nh, gg, wg):
            cs = slice(h0 * P, (h0 + nh) * P)
            nc.vector.quantize_mx(out=w_codes[:, gg, cs].bitcast(FP8X4), scales=w_scl[:, gg, cs], in_=wg[:].rearrange("p n t -> p (n t)"))

        ss_ps = ps_s.tile([P, 4, P], F32, name="ss_ps")
        ms = keep.tile([P, TT], F32, name="ms")
        rstd = keep.tile([P, TT], F32, name="rstd")

        v_of = {}
        sq_of = {}

        def open_chunk(ci):
            v_new = vpool.tile([P, H, CHUNKS[ci][1] * P], F32, name="v")
            sq_new = sqp.tile([P, H, CHUNKS[ci][1] * P], F32, name="sq")
            v_of[ci] = v_new
            sq_of[ci] = sq_new

        def mx(ci, hp):
            t0, nt = CHUNKS[ci]
            acc = ps_a.tile([P, 2, nt * P], F32, name="acc")
            ts = slice(t0 * P, (t0 + nt) * P)
            for a in range(2):
                hs = slice((2 * hp + a) * P, (2 * hp + a + 1) * P)
                for gg in range(G):
                    nc.tensor.matmul_mx(
                        out=acc[:, a, :],
                        lhsT=w_codes[:, gg, hs].bitcast(FP8X4), lhsT_scale=w_scl[:, gg, hs],
                        rhs=x_codes[:, gg, ts].bitcast(FP8X4), rhs_scale=x_scl[:, gg, ts],
                        start=(gg == 0), stop=(gg == G - 1),
                    )
            return acc

        def squares(ci, hp, acc):
            for a in range(2):
                h = 2 * hp + a
                nc.scalar.activation(out=sq_of[ci][:, h, :], in_=acc[:, a, :], func=ACT.Square, bias=bgc[:, h:h + 1])

        def values(ci, hp, acc, on_vector=False):
            for a in range(2):
                h = 2 * hp + a
                if on_vector:
                    nc.vector.tensor_scalar(out=v_of[ci][:, h, :], in0=acc[:, a, :], scalar1=bgc[:, 32 + h:33 + h], scalar2=gb[:, h:h + 1], op0=ALU.mult, op1=ALU.add)
                else:
                    nc.scalar.activation(out=v_of[ci][:, h, :], in_=acc[:, a, :], func=ACT.Identity, scale=bgc[:, 32 + h:33 + h], bias=gb[:, h:h + 1])

        def square_sum(ci, r, heads):
            for h in heads:
                nc.tensor.matmul(out=ss_ps[:, 2 * (ci % 2) + r, :], lhsT=sq_of[ci][:, h, r * P:(r + 1) * P], rhs=ident[:], is_transpose=True, start=(h == 0), stop=(h == H - 1))

        def norm(ci, r):
            i = CHUNKS[ci][0] + r
            junk = epi.tile([P, P], F32, name="junk")
            nc.scalar.activation(out=junk[:], in_=ss_ps[:, 2 * (ci % 2) + r, :], func=ACT.Copy, accum_out=ms[:, i:i + 1])
            nc.scalar.activation(out=rstd[:, i:i + 1], in_=ms[:, i:i + 1], func=ACT.Abs_reciprocal_sqrt, scale=1.0 / D, bias=eps_t[:])

        def bank_back(ci, r, q):
            bt = ps_t.tile([P, 4, J, 2], F32, name="bt", tag="tp")
            for hh in range(4):
                nc.tensor.transpose(bt[:, hh, :, :].rearrange("p j e -> p (j e)"), v_of[ci][:, 4 * q + hh, r * P:(r + 1) * P], ident[:])
            return bt

        def products(i, bt, scaled):
            t1 = epi.tile([P, 4, J, 2], F32, name="t1")
            t2 = epi.tile([P, 4, J, 2], F32, name="t2")
            cos_in = cdup[:, i * J:(i + 1) * J, :].unsqueeze(1).to_broadcast([P, 4, J, 2])
            sin_in = s3[:, i * J:(i + 1) * J, :].unsqueeze(1).to_broadcast([P, 4, J, 2])
            if scaled:
                nc.vector.scalar_tensor_tensor(out=t1[:], in0=bt[:], scalar=rstd[:, i:i + 1], in1=cos_in, op0=ALU.mult, op1=ALU.mult)
                nc.vector.scalar_tensor_tensor(out=t2[:], in0=bt[:, :, :, ::-1], scalar=rstd[:, i:i + 1], in1=sin_in, op0=ALU.mult, op1=ALU.mult)
            else:
                nc.vector.tensor_tensor(out=t1[:], in0=bt[:], in1=cos_in, op=ALU.mult)
                nc.vector.tensor_tensor(out=t2[:], in0=bt[:, :, :, ::-1], in1=sin_in, op=ALU.mult)
            return t1, t2

        def store_bank(i, q, fin):
            nc.sync.dma_start(out=out_rows[i * P:(i + 1) * P, q * NCH:(q + 1) * NCH], in_=fin[:].rearrange("p h j e -> p (h j e)"))

        o_tiles = {}

        def rope(ci, bank, bt):
            i = CHUNKS[ci][0] + bank // 3
            q = bank % 3
            if q == 0:
                o_new = epi.tile([P, H, J, 2], F32, name="o")
                o_tiles[i] = o_new
            o = o_tiles[i]
            t1, t2 = products(i, bt, True)
            nc.gpsimd.tensor_tensor(out=o[:, 4 * q:4 * q + 4, :, :], in0=t1[:], in1=t2[:], op=ALU.add)
            if q == 2:
                nc.sync.dma_start(out=out_rows[i * P:(i + 1) * P, :], in_=o[:].rearrange("p h j e -> p (h j e)"))

        def last_bank(i, q, bt, add_engine):
            t1, t2 = products(i, bt, True)
            fin = epi.tile([P, 4, J, 2], F32, name="fin")
            add_engine.tensor_tensor(out=fin[:], in0=t1[:], in1=t2[:], op=ALU.add)
            store_bank(i, q, fin)

        def keep_warm(wide, cols, n):
            dummy = ps_t.tile([P, NCH], F32, name="dummy", tag="tp")
            for t in range(n):
                nc.tensor.matmul(out=dummy[:, 0:cols], lhsT=x_sb[:, 0, 0:P], rhs=wide[:, t, :], start=True, stop=True)

        def warm_up(n):
            dummy = ps_t.tile([P, NCH], F32, name="dummy", tag="tp")
            for rep in range(n):
                nc.tensor.matmul(out=dummy[:], lhsT=x_sb[:, 0, 0:P], rhs=x_sb[:, 0, 0:NCH], start=True, stop=True)

        with tc.manual_schedule():
            for ci in range(2):
                open_chunk(ci)
            units = [(h0, nh, gg) for (h0, nh) in W_BLOCKS for gg in range(G)]
            done = set()
            mixed = None
            turned = []
            copied = []
            late_x = []
            pend = []
            sums = []
            for step in range(len(units) + 1):
                if step < len(units):
                    h0, nh, gg = units[step]
                    wide = w_widen(h0, nh, gg, 3 if step == 0 else 2 if gg == G - 1 else 1)
                new_t = [(xu, gg, x_turn(xu, gg)) for (xu, gg) in X_TURNS.get(step, ())]
                new_c = [(xu, gg, x_copy(xt)) for (xu, gg, xt) in turned]
                if step == 2:
                    bg_ps = bias_and_gain_turn()
                if step == 3:
                    bias_and_gain_copy(bg_ps)
                square_sum(0, 0, sums)
                sums = []
                if step in WARM_X:
                    warm_up(WARM_X[step])
                if mixed is not None:
                    w_quant(*mixed)
                for job in copied:
                    if job[0] < 2:
                        x_quant(*job)
                    else:
                        late_x.append(job)
                if step < len(units):
                    h0, nh, gg = units[step]
                    wg = w_mix(nh, wide)
                if step not in HOLD:
                    for (ci, hp, acc) in pend:
                        squares(ci, hp, acc)
                        values(ci, hp, acc, ci == 0 and hp in V_PAIRS)
                        done.add((ci, hp))
                        if ci == 0:
                            sums = sums + [2 * hp, 2 * hp + 1]
                    pend = []
                if mixed is not None and mixed[2] == G - 1:
                    pend = pend + [(0, hp, mx(0, hp)) for hp in range(mixed[0] // 2, (mixed[0] + mixed[1]) // 2)]
                if step == AHEAD_STEP:
                    pend.append((1, 0, mx(1, 0)))
                if step in WARM_W:
                    keep_warm(wide, units[step][1] * P, WARM_W[step])
                mixed = (h0, nh, gg, wg) if step < len(units) else None
                turned = new_t
                copied = new_c

            square_sum(0, 0, sums)
            sums = []
            copied = copied + [(xu, gg, x_copy(xt)) for (xu, gg, xt) in turned]
            ahead = [(1, hp, mx(1, hp)) for hp in (1, 2)]
            early = {q: bank_back(0, 0, q) for q in range(2)}
            for (ci, hp, acc) in pend:
                squares(ci, hp, acc)
                values(ci, hp, acc)
                done.add((ci, hp))
                if ci == 0:
                    sums = sums + [2 * hp, 2 * hp + 1]
            squares(*ahead[0])
            square_sum(0, 0, sums)
            norm(0, 0)
            values(*ahead[0])
            squares(*ahead[1])
            values(*ahead[1])
            for (ci, hp, acc) in ahead:
                done.add((ci, hp))
            for job in late_x + copied:
                x_quant(*job)
            tables()

            last = len(CHUNKS) - 1
            late = {}
            for ci in range(1, last + 1):
                if ci > 1:
                    open_chunk(ci)
                pc = ci - 1
                pair = CHUNKS[pc][1] == 2
                for cb in range(3):
                    accs = [(ci, hp, mx(ci, hp)) for hp in (2 * cb, 2 * cb + 1) if (ci, hp) not in done]
                    for a in accs[0:1]:
                        squares(*a)
                        values(*a)
                    if cb == 0 and pc > 0:
                        square_sum(pc, 0, range(8, H))
                        norm(pc, 0)
                    if cb == 1 and pair:
                        square_sum(pc, 1, range(H))
                        norm(pc, 1)
                    for a in accs[1:]:
                        squares(*a)
                        values(*a)
                    for bank in (((0, 1, 2), (3, 4), (5,)) if pair else ((0, 1), (2,), ()))[cb]:
                        rope(pc, bank, early[bank] if (pc == 0 and bank in early) else bank_back(pc, bank // 3, bank % 3))
                    if CHUNKS[ci][1] == 2 and cb == 2:
                        square_sum(ci, 0, range(8))
                    if CHUNKS[ci][1] == 1 and cb > 0:
                        square_sum(ci, 0, range(4 * cb - 4, 4 * cb))
                    if ci == last and cb == 1:
                        t1, t2 = products(TT - 1, bank_back(last, 0, 0), False)
                        un = epi.tile([P, 4, J, 2], F32, name="un")
                        nc.gpsimd.tensor_tensor(out=un[:], in0=t1[:], in1=t2[:], op=ALU.add)
                    if ci == last and cb == 2:
                        late[1] = bank_back(last, 0, 1)
            late[2] = bank_back(last, 0, 2)
            square_sum(last, 0, range(8, H))
            norm(last, 0)
            fin = epi.tile([P, 4, J, 2], F32, name="fin")
            nc.scalar.activation(out=fin[:], in_=un[:], func=ACT.Copy, scale=rstd[:, TT - 1:TT])
            store_bank(TT - 1, 0, fin)
            last_bank(TT - 1, 1, late[1], nc.gpsimd)
            last_bank(TT - 1, 2, late[2], nc.vector)
